import numpy as np
import ml_dtypes


def mxq(x, axis, fmt="e4m3"):
    dtype, down = {"e4m3": (ml_dtypes.float8_e4m3fn, 7), "e5m2": (ml_dtypes.float8_e5m2, 14)}[fmt]
    v = np.moveaxis(np.asarray(x, np.float32).astype(ml_dtypes.bfloat16).astype(np.float64), axis, -1)
    blocks = v.reshape(v.shape[:-1] + (-1, 32))
    amax = np.abs(blocks).max(-1, keepdims=True)
    byte = np.maximum(np.where(amax > 0, np.frexp(amax)[1] - 1 + 127, 0) - down, 1)
    scale = np.exp2(byte - 127.0)
    codes = (blocks / scale).astype(np.float32).astype(dtype).astype(np.float64)
    return np.moveaxis((codes * scale).reshape(v.shape), -1, axis)


WIDE = False


def mx_kscale(k):
    if not WIDE:
        return np.ones(k)
    levels = np.array([10, -10, 5, -5, 0])
    a = np.random.permutation(np.resize(levels, k // 512 * 4)).reshape(k // 512, 4)
    idx = np.arange(k)
    return np.exp2(a[idx // 512, idx % 128 // 32])


BF16 = ml_dtypes.bfloat16


def bf(x):
    return np.asarray(x, np.float32).astype(BF16)


def f64(x):
    return np.asarray(x).astype(np.float64)


B, S, P, D, H, HD = 8, 512, 512, 512, 4, 128
T = P + S


def heads(t):
    return t.reshape(B, -1, H, HD).transpose(0, 2, 1, 3)


def setup_inputs():
    s = mx_kscale(D)
    return {
        "x": bf(np.random.standard_normal((B, S, D)) * s),
        "q": bf(np.random.standard_normal((B, H, S, HD)) * 1.5),
        "k_new": bf(np.random.standard_normal((B, H, S, HD)) * 1.5),
        "past_k": bf(np.random.standard_normal((B, H, P, HD)) * 1.5),
        "past_v": bf(np.random.standard_normal((B, H, P, HD))),
        "Wv": bf(np.random.standard_normal((D, D)) / np.sqrt(D) / s[None, :]),
        "bv": bf(np.random.standard_normal(D) * 0.3),
    }


def reference(x, q, k_new, past_k, past_v, Wv, bv):
    v_new = heads((mxq(f64(x), 2, "e4m3") @ mxq(f64(Wv), 1, "e4m3").T) + f64(bv))
    v_cached = np.concatenate([f64(past_v), v_new], axis=2)
    qf = f64(q)
    scores = np.concatenate([qf @ f64(past_k).transpose(0, 1, 3, 2), qf @ f64(k_new).transpose(0, 1, 3, 2)], axis=3) * (1.0 / np.sqrt(HD))
    q_pos = np.arange(T - S, T)[:, None]
    k_pos = np.arange(T)[None, :]
    scores = np.where(q_pos >= k_pos, scores, -np.inf)
    e = np.exp(scores - scores.max(-1, keepdims=True))
    out = (mxq(e, 3, "e4m3") @ mxq(v_cached, 2, "e4m3")) / e.sum(-1, keepdims=True)
    return out.transpose(0, 2, 1, 3).reshape(B, S, D)

@@ -1,0 +1,358 @@
+import math
+from contextlib import ExitStack
+
+import concourse.mybir as mybir
+from concourse.masks import make_identity
+
+BF16 = mybir.dt.bfloat16
+F32 = mybir.dt.float32
+U32 = mybir.dt.uint32
+U8 = mybir.dt.uint8
+FP8X4 = mybir.dt.float8_e4m3fn_x4
+ALU = mybir.AluOpType
+ACT = mybir.ActivationFunctionType
+AX = mybir.AxisListType
+
+P = 128
+B, S, D, H, HD = 8, 512, 512, 4, 128
+T = 2 * S
+NT = S // P
+SCALE = 1.0 / math.sqrt(HD)
+MASK = -1.0e30
+FLOPS = 2 * B * S * D * D + 2 * 2 * B * H * S * T * HD
+
+
+def tile_flashattentionmodule_pa_t_kernel(tc, x, q, k_new, past_k, past_v, Wv, bv, out):
+    nc = tc.nc
+    with ExitStack() as ctx:
+        consts = ctx.enter_context(tc.tile_pool(name="consts", bufs=1))
+        loads = ctx.enter_context(tc.tile_pool(name="loads", bufs=2))
+        batchp = ctx.enter_context(tc.tile_pool(name="batchp", bufs=2))
+        headp = ctx.enter_context(tc.tile_pool(name="headp", bufs=2))
+        work = ctx.enter_context(tc.tile_pool(name="work", bufs=3))
+        small = ctx.enter_context(tc.tile_pool(name="small", bufs=4))
+        psum = ctx.enter_context(tc.psum_pool(name="psum", bufs=1))
+
+        ident_bf = consts.tile([P, P], BF16, name="ident_bf")
+        make_identity(nc, ident_bf[:])
+        ident_f = consts.tile([P, P], F32, name="ident_f")
+        make_identity(nc, ident_f[:])
+        mask_f = consts.tile([P, P], F32, name="mask_f")
+        nc.gpsimd.memset(mask_f[:], 0.0)
+        nc.gpsimd.affine_select(
+            out=mask_f[:], in_=mask_f[:], compare_op=ALU.is_ge, fill=MASK,
+            base=0, pattern=[[-1, P]], channel_multiplier=1,
+        )
+        mask_bf = consts.tile([P, P], BF16, name="mask_bf")
+        nc.vector.tensor_copy(out=mask_bf[:], in_=mask_f[:])
+        bias_bf = consts.tile([P, D], BF16, name="bias_bf")
+        nc.scalar.dma_start(out=bias_bf[:], in_=bv.partition_broadcast(P))
+        bias_f = consts.tile([P, D], F32, name="bias_f")
+        nc.vector.tensor_copy(out=bias_f[:], in_=bias_bf[:])
+        e_tiles = []
+        for t in range(NT):
+            e_t = consts.tile([P, T], BF16, name="e%d" % t)
+            if t < NT - 1:
+                nc.gpsimd.memset(e_t[:, S + (t + 1) * P:], 0.0)
+            e_tiles.append(e_t)
+
+        st = {}
+
+        def words_to_codes(src, grp, half, engine):
+            s32 = src[:].bitcast(F32)
+            tp = psum.tile([P, 512], F32, name="tp", tag="tr")
+            for oo in range(2):
+                for u in range(2):
+                    o = 2 * half + oo
+                    nc.tensor.transpose(
+                        tp[:, (oo * 2 + u) * P:(oo * 2 + u + 1) * P],
+                        s32[:, o * 256 + u * P:o * 256 + (u + 1) * P],
+                        ident_f[:],
+                    )
+            g32 = grp[:].bitcast(F32).rearrange("p (o m u) -> p o m u", o=4, u=2)
+            engine.tensor_copy(
+                out=g32[:, 2 * half:2 * half + 2],
+                in_=tp[:].rearrange("p (o u m) -> p o m u", o=2, u=2),
+            )
+
+        w_sb = consts.tile([P, 4 * D], BF16, name="w_sb")
+        nc.sync.dma_start(
+            out=w_sb[:].rearrange("p (o f) -> p o f", o=4),
+            in_=Wv.rearrange("(o p) f -> p o f", p=P),
+        )
+        wgrp = consts.tile([P, 4 * D], BF16, name="wgrp", align_bytes=64)
+        wcodes = consts.tile([P, D], U32, name="wcodes", align_bytes=64)
+        wscales = consts.tile([P, D], U8, name="wscales", align_bytes=64)
+
+        def load(b):
+            x_sb = loads.tile([P, 4 * D], BF16, name="x_sb")
+            xv = x_sb[:].rearrange("p (u e f) -> p u e f", u=2, e=2)
+            for u in range(2):
+                nc.sync.dma_start(
+                    out=xv[:, u],
+                    in_=x[b, 256 * u:256 * (u + 1), :].rearrange("(m e) f -> m e f", e=2),
+                )
+            pv_sb = loads.tile([P, H * S], BF16, name="pv_sb")
+            nc.sync.dma_start(
+                out=pv_sb[:].rearrange("p (h u e d) -> p h u e d", h=H, u=2, e=2),
+                in_=past_v[b].rearrange("h (u m e) d -> m h u e d", u=2, e=2),
+            )
+            pk_sb = loads.tile([P, H * S], BF16, name="pk_sb")
+            nc.sync.dma_start(
+                out=pk_sb[:].rearrange("p (h a d) -> p h a d", h=H, a=NT),
+                in_=past_k[b].rearrange("h (a p) d -> p h a d", p=P),
+            )
+            kn_sb = loads.tile([P, H * S], BF16, name="kn_sb")
+            nc.sync.dma_start(
+                out=kn_sb[:].rearrange("p (h a d) -> p h a d", h=H, a=NT),
+                in_=k_new[b].rearrange("h (a p) d -> p h a d", p=P),
+            )
+            q_sb = loads.tile([P, H * S], BF16, name="q_sb")
+            nc.sync.dma_start(
+                out=q_sb[:].rearrange("p (h a d) -> p h a d", h=H, a=NT),
+                in_=q[b].rearrange("h (a p) d -> p h a d", p=P),
+            )
+            st[("x", b)] = x_sb
+            st[("pv", b)] = pv_sb
+            st[("pk", b)] = pk_sb
+            st[("kn", b)] = kn_sb
+            st[("q", b)] = q_sb
+
+        def batch_tiles(b):
+            st[("xgrp", b)] = batchp.tile([P, 4 * D], BF16, name="xgrp", align_bytes=64)
+            st[("xcodes", b)] = batchp.tile([P, D], U32, name="xcodes", align_bytes=64)
+            st[("xscales", b)] = batchp.tile([P, D], U8, name="xscales", align_bytes=64)
+            st[("vgrp", b)] = batchp.tile([P, 2 * H * HD * 4], BF16, name="vgrp", align_bytes=64)
+            st[("vcodes", b)] = batchp.tile([P, 2 * H * HD], U32, name="vcodes", align_bytes=64)
+            st[("vscales", b)] = batchp.tile([P, 2 * H * HD], U8, name="vscales", align_bytes=64)
+            st[("o", b)] = batchp.tile([P, NT * D], F32, name="o_sb")
+
+        def x_half(b, half):
+            words_to_codes(st[("x", b)], st[("xgrp", b)], half, nc.vector)
+
+        def x_quant(b):
+            nc.vector.quantize_mx(
+                out=st[("xcodes", b)][:].bitcast(FP8X4), scales=st[("xscales", b)][:], in_=st[("xgrp", b)][:]
+            )
+
+        def pv_group(b):
+            vg = st[("vgrp", b)]
+            nc.vector.tensor_copy(
+                out=vg[:, 0:2048].rearrange("p (h d t) -> p h d t", h=H, t=4),
+                in_=st[("pv", b)][:].rearrange("p (h t d) -> p h d t", h=H, t=4),
+            )
+
+        def v_quant(b, g):
+            nc.vector.quantize_mx(
+                out=st[("vcodes", b)][:, g * 512:(g + 1) * 512].bitcast(FP8X4),
+                scales=st[("vscales", b)][:, g * 512:(g + 1) * 512],
+                in_=st[("vgrp", b)][:, g * 2048:(g + 1) * 2048],
+            )
+
+        def v_new(b, h):
+            vn = psum.tile([P, 512], F32, name="vn", tag="tr")
+            xc = st[("xcodes", b)]
+            xs = st[("xscales", b)]
+            for tau in range(4):
+                nc.tensor.matmul_mx(
+                    out=vn[:, tau * P:(tau + 1) * P],
+                    lhsT=xc[:, tau * P:(tau + 1) * P].bitcast(FP8X4),
+                    lhsT_scale=xs[:, tau * P:(tau + 1) * P],
+                    rhs=wcodes[:, h * P:(h + 1) * P].bitcast(FP8X4),
+                    rhs_scale=wscales[:, h * P:(h + 1) * P],
+                    start=True, stop=True,
+                )
+            vg = st[("vgrp", b)]
+            nc.vector.tensor_tensor(
+                out=vg[:, 2048 + h * 512:2048 + (h + 1) * 512].rearrange("p (d t) -> p d t", t=4),
+                in0=vn[:].rearrange("p (t d) -> p d t", t=4),
+                in1=bias_f[:, h * P:(h + 1) * P].unsqueeze(2).to_broadcast([P, P, 4]),
+                op=ALU.add,
+            )
+
+        def k_prep(b, h):
+            ktp = psum.tile([P, T], BF16, name="ktp", tag="tr")
+            for a in range(NT):
+                nc.tensor.transpose(
+                    ktp[:, a * P:(a + 1) * P], st[("pk", b)][:, (h * NT + a) * P:(h * NT + a + 1) * P], ident_bf[:]
+                )
+            for a in range(NT):
+                nc.tensor.transpose(
+                    ktp[:, S + a * P:S + (a + 1) * P], st[("kn", b)][:, (h * NT + a) * P:(h * NT + a + 1) * P],
+                    ident_bf[:],
+                )
+            kT = headp.tile([P, T], BF16, name="kT")
+            nc.scalar.copy(out=kT[:], in_=ktp[:])
+            st[("kT", b, h)] = kT
+
+        def q_prep(b, h):
+            qtp = psum.tile([P, S], BF16, name="qtp", tag="tr")
+            for a in range(NT):
+                nc.tensor.transpose(
+                    qtp[:, a * P:(a + 1) * P], st[("q", b)][:, (h * NT + a) * P:(h * NT + a + 1) * P], ident_bf[:]
+                )
+            qT = headp.tile([P, S], BF16, name="qT")
+            nc.scalar.copy(out=qT[:], in_=qtp[:])
+            st[("qT", b, h)] = qT
+            st[("rs", b, h)] = headp.tile([P, 2 * NT], F32, name="rs", bufs=3)
+
+        def scores(b, h, t):
+            sA = psum.tile([P, 512], F32, name="sA", bufs=2)
+            sB = psum.tile([P, 512], F32, name="sB", bufs=2)
+            kT = st[("kT", b, h)]
+            lq = st[("qT", b, h)][:, t * P:(t + 1) * P]
+            nc.tensor.matmul(sA[:], lhsT=lq, rhs=kT[:, 0:S], start=True, stop=True)
+            if t > 0:
+                nc.tensor.matmul(sB[:, 0:t * P], lhsT=lq, rhs=kT[:, S:S + t * P], start=True, stop=True)
+            nc.tensor.matmul(
+                sB[:, t * P:(t + 1) * P], lhsT=lq, rhs=kT[:, S + t * P:S + (t + 1) * P], start=True, stop=False
+            )
+            nc.tensor.matmul(sB[:, t * P:(t + 1) * P], lhsT=ident_bf[:], rhs=mask_bf[:], start=False, stop=True)
+            st[("sA", b, h, t)] = sA
+            st[("sB", b, h, t)] = sB
+
+        def rowmax(b, h, t):
+            mx = small.tile([P, 2], F32, name="mx")
+            nc.vector.tensor_reduce(out=mx[:, 0:1], in_=st[("sA", b, h, t)][:], axis=AX.X, op=ALU.max, negate=True)
+            nc.vector.tensor_reduce(
+                out=mx[:, 1:2], in_=st[("sB", b, h, t)][:, 0:(t + 1) * P], axis=AX.X, op=ALU.max, negate=True
+            )
+            nb = small.tile([P, 1], F32, name="nb")
+            nc.vector.tensor_scalar(
+                out=nb[:], in0=mx[:, 0:1], scalar1=mx[:, 1:2], scalar2=SCALE, op0=ALU.min, op1=ALU.mult
+            )
+            st[("nb", b, h, t)] = nb
+
+        def expo(b, h, t):
+            e_t = e_tiles[t]
+            nb = st[("nb", b, h, t)]
+            rs = st[("rs", b, h)]
+            nc.scalar.activation(
+                out=e_t[:, 0:S], in_=st[("sA", b, h, t)][:], func=ACT.Exp, bias=nb[:], scale=SCALE,
+                accum_out=rs[:, 2 * t:2 * t + 1],
+            )
+            nc.scalar.activation(
+                out=e_t[:, S:S + (t + 1) * P], in_=st[("sB", b, h, t)][:, 0:(t + 1) * P], func=ACT.Exp,
+                bias=nb[:], scale=SCALE, accum_out=rs[:, 2 * t + 1:2 * t + 2],
+            )
+
+        def e_transpose(b, h, t):
+            eT = psum.tile([P, 512], F32, name="eT", bufs=2)
+            e32 = e_tiles[t][:].bitcast(F32)
+            for j in range(4):
+                nc.tensor.transpose(eT[:, j * P:(j + 1) * P], e32[:, j * P:(j + 1) * P], ident_f[:])
+            st[("eT", b, h, t)] = eT
+
+        def e_evac(b, h, t):
+            egrp = work.tile([P, T], BF16, name="egrp", align_bytes=64)
+            nc.scalar.copy(
+                out=egrp[:].bitcast(F32).rearrange("p (g m u) -> p g m u", g=2, u=2),
+                in_=st[("eT", b, h, t)][:].rearrange("p (g u m) -> p g m u", g=2, u=2),
+            )
+            st[("egrp", b, h, t)] = egrp
+
+        def e_quant(b, h, t):
+            ec = work.tile([P, 256], U32, name="ec", align_bytes=64)
+            es = work.tile([P, 256], U8, name="es", align_bytes=64)
+            nc.vector.quantize_mx(out=ec[:].bitcast(FP8X4), scales=es[:], in_=st[("egrp", b, h, t)][:])
+            st[("ec", b, h, t)] = ec
+            st[("es", b, h, t)] = es
+
+        def pv(b, h, t):
+            if t == 0:
+                st[("ops", b, h)] = psum.tile([P, 512], F32, name="ops")
+            ops = st[("ops", b, h)]
+            ec = st[("ec", b, h, t)]
+            es = st[("es", b, h, t)]
+            vc = st[("vcodes", b)]
+            vs = st[("vscales", b)]
+            for g in range(2):
+                c0 = (g * H + h) * P
+                nc.tensor.matmul_mx(
+                    out=ops[:, t * P:(t + 1) * P],
+                    lhsT=ec[:, g * P:(g + 1) * P].bitcast(FP8X4),
+                    lhsT_scale=es[:, g * P:(g + 1) * P],
+                    rhs=vc[:, c0:c0 + P].bitcast(FP8X4),
+                    rhs_scale=vs[:, c0:c0 + P],
+                    start=(g == 0), stop=(g == 1),
+                )
+
+        def finish_head(b, h):
+            rsum = small.tile([P, NT], F32, name="rsum")
+            nc.vector.tensor_reduce(
+                out=rsum[:], in_=st[("rs", b, h)][:].rearrange("p (t j) -> p t j", j=2), axis=AX.X, op=ALU.add
+            )
+            rc = small.tile([P, NT], F32, name="rc")
+            nc.vector.reciprocal(out=rc[:], in_=rsum[:])
+            nc.vector.tensor_tensor(
+                out=st[("o", b)][:].rearrange("p (t h d) -> p t h d", t=NT, h=H)[:, :, h, :],
+                in0=st[("ops", b, h)][:].rearrange("p (t d) -> p t d", t=NT),
+                in1=rc[:].unsqueeze(2).to_broadcast([P, NT, P]),
+                op=ALU.mult,
+            )
+            if h == H - 1:
+                nc.sync.dma_start(
+                    out=out[b].rearrange("(t p) c -> p t c", p=P),
+                    in_=st[("o", b)][:].rearrange("p (t c) -> p t c", t=NT),
+                )
+
+        load(0)
+        for half in range(2):
+            words_to_codes(w_sb, wgrp, half, nc.vector)
+        nc.vector.quantize_mx(out=wcodes[:].bitcast(FP8X4), scales=wscales[:], in_=wgrp[:])
+        batch_tiles(0)
+        k_prep(0, 0)
+        q_prep(0, 0)
+        x_half(0, 0)
+        x_half(0, 1)
+        pv_group(0)
+        x_quant(0)
+        v_quant(0, 0)
+        for h in range(H):
+            v_new(0, h)
+        v_quant(0, 1)
+
+        steps = [(b, h, t) for b in range(B) for h in range(H) for t in range(NT)]
+        n_steps = len(steps)
+        scores(*steps[0])
+        rowmax(*steps[0])
+        for n in range(n_steps + 2):
+            if n >= 2:
+                e_quant(*steps[n - 2])
+            if n + 1 < n_steps:
+                scores(*steps[n + 1])
+                rowmax(*steps[n + 1])
+            if n < n_steps:
+                expo(*steps[n])
+            if 1 <= n <= n_steps:
+                e_transpose(*steps[n - 1])
+                e_evac(*steps[n - 1])
+            if n >= 2:
+                pb, ph, pt = steps[n - 2]
+                pv(pb, ph, pt)
+                if pt == NT - 1:
+                    finish_head(pb, ph)
+            if n < n_steps:
+                b, h, t = steps[n]
+                b2, h2 = (b, h + 1) if h + 1 < H else (b + 1, 0)
+                if h == 0 and t == 0 and b + 1 < B:
+                    load(b + 1)
+                if b2 < B and t == 0:
+                    k_prep(b2, h2)
+                if b2 < B and t == 1:
+                    q_prep(b2, h2)
+                if b + 1 < B and t >= 2:
+                    item = 2 * h + (t - 2)
+                    if item == 0:
+                        batch_tiles(b + 1)
+                    if item < 2:
+                        x_half(b + 1, item)
+                    if item == 1:
+                        pv_group(b + 1)
+                    if item == 2:
+                        x_quant(b + 1)
+                        v_quant(b + 1, 0)
+                    if 2 <= item < 6:
+                        v_new(b + 1, item - 2)
+                    if item == 6:
+                        v_quant(b + 1, 1)

@@ -11,7 +11,6 @@ U8 = mybir.dt.uint8
 FP8X4 = mybir.dt.float8_e4m3fn_x4
 ALU = mybir.AluOpType
 ACT = mybir.ActivationFunctionType
-AX = mybir.AxisListType
 
 P = 128
 B, S, D, H, HD = 8, 512, 512, 4, 128
@@ -20,6 +19,8 @@ NT = S // P
 SCALE = 1.0 / math.sqrt(HD)
 MASK = -1.0e30
 FLOPS = 2 * B * S * D * D + 2 * 2 * B * H * S * T * HD
+PSUM_BUFS = {"tr": 1, "ops": 1, "eT": 2}
+E_ON_VECTOR = ()
 
 
 def tile_flashattentionmodule_pa_t_kernel(tc, x, q, k_new, past_k, past_v, Wv, bv, out):
@@ -27,16 +28,50 @@ def tile_flashattentionmodule_pa_t_kernel(tc, x, q, k_new, past_k, past_v, Wv, b
     with ExitStack() as ctx:
         consts = ctx.enter_context(tc.tile_pool(name="consts", bufs=1))
         loads = ctx.enter_context(tc.tile_pool(name="loads", bufs=2))
-        batchp = ctx.enter_context(tc.tile_pool(name="batchp", bufs=2))
+        batchp = ctx.enter_context(tc.tile_pool(name="batchp", bufs=3))
         headp = ctx.enter_context(tc.tile_pool(name="headp", bufs=2))
         work = ctx.enter_context(tc.tile_pool(name="work", bufs=3))
-        small = ctx.enter_context(tc.tile_pool(name="small", bufs=4))
+        small = ctx.enter_context(tc.tile_pool(name="small", bufs=6))
         psum = ctx.enter_context(tc.psum_pool(name="psum", bufs=1))
+        ctx.enter_context(tc.manual_schedule())
 
+        st = {}
+
+        def load_qk(b, h0, h1):
+            for key, src in (("pk", past_k), ("kn", k_new), ("q", q)):
+                nc.sync.dma_start(
+                    out=st[(key, b)][:, h0 * S:h1 * S].rearrange("p (h a d) -> p h a d", h=h1 - h0, a=NT),
+                    in_=src[b, h0:h1].rearrange("h (a p) d -> p h a d", p=P),
+                )
+
+        def load_xv(b):
+            xv = st[("x", b)][:].rearrange("p (u e f) -> p u e f", u=2, e=2)
+            for u in range(2):
+                nc.sync.dma_start(
+                    out=xv[:, u],
+                    in_=x[b, 256 * u:256 * (u + 1), :].rearrange("(m e) f -> m e f", e=2),
+                )
+            nc.sync.dma_start(
+                out=st[("pv", b)][:].rearrange("p (h u e d) -> p h u e d", h=H, u=2, e=2),
+                in_=past_v[b].rearrange("h (u m e) d -> m h u e d", u=2, e=2),
+            )
+
+        def load_tiles(b):
+            for key in ("x", "pv", "pk", "kn", "q"):
+                st[(key, b)] = loads.tile([P, H * S], BF16, name=key + "_sb")
+
+        load_tiles(0)
+        load_qk(0, 0, 1)
+        load_qk(0, 1, 2)
+        w_sb = consts.tile([P, 4 * D], BF16, name="w_sb")
+        nc.sync.dma_start(
+            out=w_sb[:].rearrange("p (o f) -> p o f", o=4),
+            in_=Wv.rearrange("(o p) f -> p o f", p=P),
+        )
+        load_xv(0)
+        load_qk(0, 2, H)
         ident_bf = consts.tile([P, P], BF16, name="ident_bf")
         make_identity(nc, ident_bf[:])
-        ident_f = consts.tile([P, P], F32, name="ident_f")
-        make_identity(nc, ident_f[:])
         mask_f = consts.tile([P, P], F32, name="mask_f")
         nc.gpsimd.memset(mask_f[:], 0.0)
         nc.gpsimd.affine_select(
@@ -45,22 +80,27 @@ def tile_flashattentionmodule_pa_t_kernel(tc, x, q, k_new, past_k, past_v, Wv, b
         )
         mask_bf = consts.tile([P, P], BF16, name="mask_bf")
         nc.vector.tensor_copy(out=mask_bf[:], in_=mask_f[:])
-        bias_bf = consts.tile([P, D], BF16, name="bias_bf")
-        nc.scalar.dma_start(out=bias_bf[:], in_=bv.partition_broadcast(P))
-        bias_f = consts.tile([P, D], F32, name="bias_f")
-        nc.vector.tensor_copy(out=bias_f[:], in_=bias_bf[:])
+        ident_f = consts.tile([P, P], F32, name="ident_f")
+        make_identity(nc, ident_f[:])
         e_tiles = []
         for t in range(NT):
             e_t = consts.tile([P, T], BF16, name="e%d" % t)
             if t < NT - 1:
                 nc.gpsimd.memset(e_t[:, S + (t + 1) * P:], 0.0)
             e_tiles.append(e_t)
+        bias_bf = consts.tile([P, D], BF16, name="bias_bf")
+        nc.gpsimd.memset(bias_bf[:], 0.0)
+        nc.sync.dma_start(out=bias_bf[0:1, :], in_=bv.rearrange("(o n) -> o n", o=1))
+        ones_bf = consts.tile([P, P], BF16, name="ones_bf")
+        nc.gpsimd.memset(ones_bf[:], 1.0)
+        bias_f = consts.tile([P, D], F32, name="bias_f")
+        wgrp = consts.tile([P, 4 * D], BF16, name="wgrp", align_bytes=64)
+        wcodes = consts.tile([P, D], U32, name="wcodes", align_bytes=64)
+        wscales = consts.tile([P, D], U8, name="wscales", align_bytes=64)
 
-        st = {}
-
-        def words_to_codes(src, grp, half, engine):
+        def words_pe(src, half):
             s32 = src[:].bitcast(F32)
-            tp = psum.tile([P, 512], F32, name="tp", tag="tr")
+            tp = psum.tile([P, 512], F32, name="tp", tag="ops")
             for oo in range(2):
                 for u in range(2):
                     o = 2 * half + oo
@@ -69,54 +109,14 @@ def tile_flashattentionmodule_pa_t_kernel(tc, x, q, k_new, past_k, past_v, Wv, b
                         s32[:, o * 256 + u * P:o * 256 + (u + 1) * P],
                         ident_f[:],
                     )
+            return tp
+
+        def words_out(tp, grp, half):
             g32 = grp[:].bitcast(F32).rearrange("p (o m u) -> p o m u", o=4, u=2)
-            engine.tensor_copy(
+            nc.vector.tensor_copy(
                 out=g32[:, 2 * half:2 * half + 2],
                 in_=tp[:].rearrange("p (o u m) -> p o m u", o=2, u=2),
             )
-
-        w_sb = consts.tile([P, 4 * D], BF16, name="w_sb")
-        nc.sync.dma_start(
-            out=w_sb[:].rearrange("p (o f) -> p o f", o=4),
-            in_=Wv.rearrange("(o p) f -> p o f", p=P),
-        )
-        wgrp = consts.tile([P, 4 * D], BF16, name="wgrp", align_bytes=64)
-        wcodes = consts.tile([P, D], U32, name="wcodes", align_bytes=64)
-        wscales = consts.tile([P, D], U8, name="wscales", align_bytes=64)
-
-        def load(b):
-            x_sb = loads.tile([P, 4 * D], BF16, name="x_sb")
-            xv = x_sb[:].rearrange("p (u e f) -> p u e f", u=2, e=2)
-            for u in range(2):
-                nc.sync.dma_start(
-                    out=xv[:, u],
-                    in_=x[b, 256 * u:256 * (u + 1), :].rearrange("(m e) f -> m e f", e=2),
-                )
-            pv_sb = loads.tile([P, H * S], BF16, name="pv_sb")
-            nc.sync.dma_start(
-                out=pv_sb[:].rearrange("p (h u e d) -> p h u e d", h=H, u=2, e=2),
-                in_=past_v[b].rearrange("h (u m e) d -> m h u e d", u=2, e=2),
-            )
-            pk_sb = loads.tile([P, H * S], BF16, name="pk_sb")
-            nc.sync.dma_start(
-                out=pk_sb[:].rearrange("p (h a d) -> p h a d", h=H, a=NT),
-                in_=past_k[b].rearrange("h (a p) d -> p h a d", p=P),
-            )
-            kn_sb = loads.tile([P, H * S], BF16, name="kn_sb")
-            nc.sync.dma_start(
-                out=kn_sb[:].rearrange("p (h a d) -> p h a d", h=H, a=NT),
-                in_=k_new[b].rearrange("h (a p) d -> p h a d", p=P),
-            )
-            q_sb = loads.tile([P, H * S], BF16, name="q_sb")
-            nc.sync.dma_start(
-                out=q_sb[:].rearrange("p (h a d) -> p h a d", h=H, a=NT),
-                in_=q[b].rearrange("h (a p) d -> p h a d", p=P),
-            )
-            st[("x", b)] = x_sb
-            st[("pv", b)] = pv_sb
-            st[("pk", b)] = pk_sb
-            st[("kn", b)] = kn_sb
-            st[("q", b)] = q_sb
 
         def batch_tiles(b):
             st[("xgrp", b)] = batchp.tile([P, 4 * D], BF16, name="xgrp", align_bytes=64)
@@ -125,22 +125,17 @@ def tile_flashattentionmodule_pa_t_kernel(tc, x, q, k_new, past_k, past_v, Wv, b
             st[("vgrp", b)] = batchp.tile([P, 2 * H * HD * 4], BF16, name="vgrp", align_bytes=64)
             st[("vcodes", b)] = batchp.tile([P, 2 * H * HD], U32, name="vcodes", align_bytes=64)
             st[("vscales", b)] = batchp.tile([P, 2 * H * HD], U8, name="vscales", align_bytes=64)
-            st[("o", b)] = batchp.tile([P, NT * D], F32, name="o_sb")
-
-        def x_half(b, half):
-            words_to_codes(st[("x", b)], st[("xgrp", b)], half, nc.vector)
 
         def x_quant(b):
             nc.vector.quantize_mx(
                 out=st[("xcodes", b)][:].bitcast(FP8X4), scales=st[("xscales", b)][:], in_=st[("xgrp", b)][:]
             )
 
-        def pv_group(b):
+        def pv_group(b, h):
             vg = st[("vgrp", b)]
-            nc.vector.tensor_copy(
-                out=vg[:, 0:2048].rearrange("p (h d t) -> p h d t", h=H, t=4),
-                in_=st[("pv", b)][:].rearrange("p (h t d) -> p h d t", h=H, t=4),
-            )
+            dst = vg[:, h * 512:(h + 1) * 512].rearrange("p (d t) -> p d t", t=4)
+            src = st[("pv", b)][:, h * 512:(h + 1) * 512].rearrange("p (t d) -> p d t", t=4)
+            nc.gpsimd.tensor_scalar(out=dst, in0=src, scalar1=1.0, scalar2=0.0, op0=ALU.mult, op1=ALU.add)
 
         def v_quant(b, g):
             nc.vector.quantize_mx(
@@ -149,8 +144,8 @@ def tile_flashattentionmodule_pa_t_kernel(tc, x, q, k_new, past_k, past_v, Wv, b
                 in_=st[("vgrp", b)][:, g * 2048:(g + 1) * 2048],
             )
 
-        def v_new(b, h):
-            vn = psum.tile([P, 512], F32, name="vn", tag="tr")
+        def vnew_pe(b, h):
+            vn = psum.tile([P, 512], F32, name="vn", tag="ops")
             xc = st[("xcodes", b)]
             xs = st[("xscales", b)]
             for tau in range(4):
@@ -162,6 +157,9 @@ def tile_flashattentionmodule_pa_t_kernel(tc, x, q, k_new, past_k, past_v, Wv, b
                     rhs_scale=wscales[:, h * P:(h + 1) * P],
                     start=True, stop=True,
                 )
+            return vn
+
+        def vnew_out(vn, b, h):
             vg = st[("vgrp", b)]
             nc.vector.tensor_tensor(
                 out=vg[:, 2048 + h * 512:2048 + (h + 1) * 512].rearrange("p (d t) -> p d t", t=4),
@@ -170,8 +168,8 @@ def tile_flashattentionmodule_pa_t_kernel(tc, x, q, k_new, past_k, past_v, Wv, b
                 op=ALU.add,
             )
 
-        def k_prep(b, h):
-            ktp = psum.tile([P, T], BF16, name="ktp", tag="tr")
+        def k_pe(b, h, tag="tr"):
+            ktp = psum.tile([P, T], BF16, name="ktp", tag=tag, bufs=PSUM_BUFS[tag])
             for a in range(NT):
                 nc.tensor.transpose(
                     ktp[:, a * P:(a + 1) * P], st[("pk", b)][:, (h * NT + a) * P:(h * NT + a + 1) * P], ident_bf[:]
@@ -181,20 +179,26 @@ def tile_flashattentionmodule_pa_t_kernel(tc, x, q, k_new, past_k, past_v, Wv, b
                     ktp[:, S + a * P:S + (a + 1) * P], st[("kn", b)][:, (h * NT + a) * P:(h * NT + a + 1) * P],
                     ident_bf[:],
                 )
+            st[("ktp", b, h)] = ktp
+
+        def k_out(b, h):
             kT = headp.tile([P, T], BF16, name="kT")
-            nc.scalar.copy(out=kT[:], in_=ktp[:])
+            nc.scalar.copy(out=kT[:], in_=st[("ktp", b, h)][:])
             st[("kT", b, h)] = kT
 
-        def q_prep(b, h):
-            qtp = psum.tile([P, S], BF16, name="qtp", tag="tr")
+        def q_pe(b, h, tag="tr"):
+            qtp = psum.tile([P, S], BF16, name="qtp", tag=tag, bufs=PSUM_BUFS[tag])
             for a in range(NT):
                 nc.tensor.transpose(
                     qtp[:, a * P:(a + 1) * P], st[("q", b)][:, (h * NT + a) * P:(h * NT + a + 1) * P], ident_bf[:]
                 )
+            st[("qtp", b, h)] = qtp
+
+        def q_out(b, h, copy_fn=nc.scalar.copy):
             qT = headp.tile([P, S], BF16, name="qT")
-            nc.scalar.copy(out=qT[:], in_=qtp[:])
+            copy_fn(out=qT[:], in_=st[("qtp", b, h)][:])
             st[("qT", b, h)] = qT
-            st[("rs", b, h)] = headp.tile([P, 2 * NT], F32, name="rs", bufs=3)
+            st[("rs", b, h)] = headp.tile([P, NT], F32, name="rs", bufs=8)
 
         def scores(b, h, t):
             sA = psum.tile([P, 512], F32, name="sA", bufs=2)
@@ -212,147 +216,204 @@ def tile_flashattentionmodule_pa_t_kernel(tc, x, q, k_new, past_k, past_v, Wv, b
             st[("sB", b, h, t)] = sB
 
         def rowmax(b, h, t):
-            mx = small.tile([P, 2], F32, name="mx")
-            nc.vector.tensor_reduce(out=mx[:, 0:1], in_=st[("sA", b, h, t)][:], axis=AX.X, op=ALU.max, negate=True)
-            nc.vector.tensor_reduce(
-                out=mx[:, 1:2], in_=st[("sB", b, h, t)][:, 0:(t + 1) * P], axis=AX.X, op=ALU.max, negate=True
-            )
+            w = (t + 1) * P
+            sc = work.tile([P, T], F32, name="sc", bufs=4)
+            a0 = small.tile([P, 1], F32, name="a0")
             nb = small.tile([P, 1], F32, name="nb")
             nc.vector.tensor_scalar(
-                out=nb[:], in0=mx[:, 0:1], scalar1=mx[:, 1:2], scalar2=SCALE, op0=ALU.min, op1=ALU.mult
+                out=sc[:, 0:S], in0=st[("sA", b, h, t)][:], scalar1=-SCALE, scalar2=None,
+                op0=ALU.mult, op1=ALU.min, accum_out=a0[:],
             )
+            nc.vector.tensor_scalar(
+                out=sc[:, S:S + w], in0=st[("sB", b, h, t)][:, 0:w], scalar1=-SCALE, scalar2=a0[:],
+                op0=ALU.mult, op1=ALU.min, accum_out=nb[:],
+            )
+            st[("sc", b, h, t)] = sc
             st[("nb", b, h, t)] = nb
 
         def expo(b, h, t):
-            e_t = e_tiles[t]
-            nb = st[("nb", b, h, t)]
-            rs = st[("rs", b, h)]
+            w = S + (t + 1) * P
             nc.scalar.activation(
-                out=e_t[:, 0:S], in_=st[("sA", b, h, t)][:], func=ACT.Exp, bias=nb[:], scale=SCALE,
-                accum_out=rs[:, 2 * t:2 * t + 1],
-            )
-            nc.scalar.activation(
-                out=e_t[:, S:S + (t + 1) * P], in_=st[("sB", b, h, t)][:, 0:(t + 1) * P], func=ACT.Exp,
-                bias=nb[:], scale=SCALE, accum_out=rs[:, 2 * t + 1:2 * t + 2],
+                out=e_tiles[t][:, 0:w], in_=st[("sc", b, h, t)][:, 0:w], func=ACT.Exp,
+                bias=st[("nb", b, h, t)][:], scale=-1.0, accum_out=st[("rs", b, h)][:, t:t + 1],
             )
 
-        def e_transpose(b, h, t):
+        def e_pe(b, h, t):
             eT = psum.tile([P, 512], F32, name="eT", bufs=2)
             e32 = e_tiles[t][:].bitcast(F32)
             for j in range(4):
                 nc.tensor.transpose(eT[:, j * P:(j + 1) * P], e32[:, j * P:(j + 1) * P], ident_f[:])
             st[("eT", b, h, t)] = eT
 
-        def e_evac(b, h, t):
-            egrp = work.tile([P, T], BF16, name="egrp", align_bytes=64)
-            nc.scalar.copy(
-                out=egrp[:].bitcast(F32).rearrange("p (g m u) -> p g m u", g=2, u=2),
-                in_=st[("eT", b, h, t)][:].rearrange("p (g u m) -> p g m u", g=2, u=2),
-            )
+        def e_out(b, h, t):
+            egrp = work.tile([P, T], BF16, name="egrp", align_bytes=64, bufs=4)
+            dst = egrp[:].bitcast(F32).rearrange("p (g m u) -> p g m u", g=2, u=2)
+            src = st[("eT", b, h, t)][:].rearrange("p (g u m) -> p g m u", g=2, u=2)
+            if (h % 2, t) in E_ON_VECTOR:
+                nc.vector.tensor_copy(out=dst, in_=src)
+            else:
+                nc.scalar.copy(out=dst, in_=src)
             st[("egrp", b, h, t)] = egrp
 
         def e_quant(b, h, t):
-            ec = work.tile([P, 256], U32, name="ec", align_bytes=64)
-            es = work.tile([P, 256], U8, name="es", align_bytes=64)
+            ec = work.tile([P, 256], U32, name="ec", align_bytes=64, bufs=16)
+            es = work.tile([P, 256], U8, name="es", align_bytes=64, bufs=16)
             nc.vector.quantize_mx(out=ec[:].bitcast(FP8X4), scales=es[:], in_=st[("egrp", b, h, t)][:])
             st[("ec", b, h, t)] = ec
             st[("es", b, h, t)] = es
 
-        def pv(b, h, t):
-            if t == 0:
-                st[("ops", b, h)] = psum.tile([P, 512], F32, name="ops")
-            ops = st[("ops", b, h)]
-            ec = st[("ec", b, h, t)]
-            es = st[("es", b, h, t)]
+        def pv_pair(b, h, t0):
+            ops = psum.tile([P, 512], F32, name="ops")
             vc = st[("vcodes", b)]
             vs = st[("vscales", b)]
-            for g in range(2):
-                c0 = (g * H + h) * P
-                nc.tensor.matmul_mx(
-                    out=ops[:, t * P:(t + 1) * P],
-                    lhsT=ec[:, g * P:(g + 1) * P].bitcast(FP8X4),
-                    lhsT_scale=es[:, g * P:(g + 1) * P],
-                    rhs=vc[:, c0:c0 + P].bitcast(FP8X4),
-                    rhs_scale=vs[:, c0:c0 + P],
-                    start=(g == 0), stop=(g == 1),
-                )
+            for t in (t0, t0 + 1):
+                ec = st[("ec", b, h, t)]
+                es = st[("es", b, h, t)]
+                for g in range(2):
+                    c0 = (g * H + h) * P
+                    nc.tensor.matmul_mx(
+                        out=ops[:, (t - t0) * P:(t - t0 + 1) * P],
+                        lhsT=ec[:, g * P:(g + 1) * P].bitcast(FP8X4),
+                        lhsT_scale=es[:, g * P:(g + 1) * P],
+                        rhs=vc[:, c0:c0 + P].bitcast(FP8X4),
+                        rhs_scale=vs[:, c0:c0 + P],
+                        start=(g == 0), stop=(g == 1),
+                    )
+            return ops
 
-        def finish_head(b, h):
-            rsum = small.tile([P, NT], F32, name="rsum")
-            nc.vector.tensor_reduce(
-                out=rsum[:], in_=st[("rs", b, h)][:].rearrange("p (t j) -> p t j", j=2), axis=AX.X, op=ALU.add
-            )
-            rc = small.tile([P, NT], F32, name="rc")
-            nc.vector.reciprocal(out=rc[:], in_=rsum[:])
+        def finish_pair(ops, b, h, t0):
+            rc = small.tile([P, 2], F32, name="rc")
+            nc.vector.reciprocal(out=rc[:], in_=st[("rs", b, h)][:, t0:t0 + 2])
+            if t0 == 0:
+                st[("o", b, h)] = work.tile([P, NT * P], F32, name="o_sb")
+            o_sb = st[("o", b, h)]
             nc.vector.tensor_tensor(
-                out=st[("o", b)][:].rearrange("p (t h d) -> p t h d", t=NT, h=H)[:, :, h, :],
-                in0=st[("ops", b, h)][:].rearrange("p (t d) -> p t d", t=NT),
-                in1=rc[:].unsqueeze(2).to_broadcast([P, NT, P]),
+                out=o_sb[:, t0 * P:(t0 + 2) * P].rearrange("p (t d) -> p t d", t=2),
+                in0=ops[:, 0:2 * P].rearrange("p (t d) -> p t d", t=2),
+                in1=rc[:].unsqueeze(2).to_broadcast([P, 2, P]),
                 op=ALU.mult,
             )
-            if h == H - 1:
+            last = b == B - 1 and h == H - 1
+            if t0 == 2 and not last:
                 nc.sync.dma_start(
-                    out=out[b].rearrange("(t p) c -> p t c", p=P),
-                    in_=st[("o", b)][:].rearrange("p (t c) -> p t c", t=NT),
+                    out=out[b, :, h * P:(h + 1) * P].rearrange("(t p) d -> p t d", p=P),
+                    in_=o_sb[:].rearrange("p (t d) -> p t d", t=NT),
+                )
+            if last:
+                nc.sync.dma_start(
+                    out=out[b, t0 * P:(t0 + 2) * P, h * P:(h + 1) * P].rearrange("(t p) d -> p t d", p=P),
+                    in_=o_sb[:, t0 * P:(t0 + 2) * P].rearrange("p (t d) -> p t d", t=2),
                 )
 
-        load(0)
-        for half in range(2):
-            words_to_codes(w_sb, wgrp, half, nc.vector)
-        nc.vector.quantize_mx(out=wcodes[:].bitcast(FP8X4), scales=wscales[:], in_=wgrp[:])
-        batch_tiles(0)
-        k_prep(0, 0)
-        q_prep(0, 0)
-        x_half(0, 0)
-        x_half(0, 1)
-        pv_group(0)
-        x_quant(0)
-        v_quant(0, 0)
-        for h in range(H):
-            v_new(0, h)
-        v_quant(0, 1)
-
-        steps = [(b, h, t) for b in range(B) for h in range(H) for t in range(NT)]
+        heads = [(b, h) for b in range(B) for h in range(H)]
+        steps = [(b, h, t) for (b, h) in heads for t in range(NT)]
         n_steps = len(steps)
-        scores(*steps[0])
-        rowmax(*steps[0])
-        for n in range(n_steps + 2):
-            if n >= 2:
-                e_quant(*steps[n - 2])
-            if n + 1 < n_steps:
-                scores(*steps[n + 1])
-                rowmax(*steps[n + 1])
+
+        def bias_pe():
+            bp = psum.tile([P, 512], F32, name="bp", tag="ops")
+            nc.tensor.matmul(bp[:], lhsT=ones_bf[:], rhs=bias_bf[:], start=True, stop=True)
+            return bp
+
+        def value_jobs(b):
+            return [("x", b, 0), ("x", b, 1), ("vn", b, 0), ("vn", b, 1), ("vn", b, 2), ("vn", b, 3)]
+
+        jobs = [("w", 0, 0), ("w", 0, 1), ("x", 0, 0), ("x", 0, 1), ("bias", 0, 0)] + value_jobs(0)[2:]
+        for b in range(B):
+            nxt = value_jobs(b + 1) if b + 1 < B else []
+            for j in range(2 * H):
+                jobs.append(("pair", b, j))
+                if j in (0, 1, 3, 4, 5, 6) and nxt:
+                    jobs.append(nxt.pop(0))
+
+        def run_job(job, outs, late):
+            kind, b, j = job
+            if kind == "w":
+                tp = words_pe(w_sb, j)
+                outs.append(lambda: words_out(tp, wgrp, j))
+                if j == 1:
+                    late.append(lambda: nc.vector.quantize_mx(
+                        out=wcodes[:].bitcast(FP8X4), scales=wscales[:], in_=wgrp[:]))
+            if kind == "x":
+                if j == 0 and b > 0:
+                    batch_tiles(b)
+                    for h in range(H):
+                        pv_group(b, h)
+                tp = words_pe(st[("x", b)], j)
+                outs.append(lambda: words_out(tp, st[("xgrp", b)], j))
+                if j == 1:
+                    late.append(lambda: x_quant(b))
+                    late.append(lambda: v_quant(b, 0))
+            if kind == "bias":
+                bp = bias_pe()
+                outs.append(lambda: nc.vector.tensor_copy(out=bias_f[:], in_=bp[:]))
+            if kind == "vn":
+                vn = vnew_pe(b, j)
+                outs.append(lambda: vnew_out(vn, b, j))
+                if j == H - 1:
+                    late.append(lambda: v_quant(b, 1))
+            if kind == "pair":
+                ops = pv_pair(b, j // 2, 2 * (j % 2))
+                outs.append(lambda: finish_pair(ops, b, j // 2, 2 * (j % 2)))
+
+        def job_ready(job, n):
+            kind, b, j = job
+            if kind != "pair":
+                return True
+            return (b * 2 * H + j) * 2 + 1 + 4 <= n
+
+        batch_tiles(0)
+        k_pe(0, 0, "tr")
+        q_pe(0, 0, "ops")
+        k_out(0, 0)
+        q_out(0, 0, nc.vector.tensor_copy)
+        k_pe(0, 1, "eT")
+        q_pe(0, 1, "eT")
+        k_out(0, 1)
+        q_out(0, 1, nc.vector.tensor_copy)
+        for n in range(2):
+            scores(*steps[n])
+            rowmax(*steps[n])
+        for h in range(H):
+            pv_group(0, h)
+
+        late = []
+        for n in range(n_steps + 4 + 40):
+            if n >= n_steps + 3 and not jobs and not late:
+                break
+            now = late
+            late = []
+            outs = []
+            b, h, t = steps[min(n, n_steps - 1)]
+            hi = heads.index((b, h))
+            for fn in now:
+                fn()
+            if 0 <= n - 3 < n_steps:
+                e_quant(*steps[n - 3])
+            for part in ("A", "D", "J", "K"):
+                if part == "A" and n + 2 < n_steps:
+                    scores(*steps[n + 2])
+                    rowmax(*steps[n + 2])
+                if part == "D" and 0 <= n - 1 < n_steps:
+                    e_pe(*steps[n - 1])
+                if part == "J" and jobs and job_ready(jobs[0], n):
+                    run_job(jobs.pop(0), outs, late)
+                if part == "K" and n < n_steps and hi + 2 < len(heads):
+                    if t == 1:
+                        k_pe(*heads[hi + 2])
+                    if t == 3:
+                        q_pe(*heads[hi + 2])
             if n < n_steps:
                 expo(*steps[n])
-            if 1 <= n <= n_steps:
-                e_transpose(*steps[n - 1])
-                e_evac(*steps[n - 1])
-            if n >= 2:
-                pb, ph, pt = steps[n - 2]
-                pv(pb, ph, pt)
-                if pt == NT - 1:
-                    finish_head(pb, ph)
+            if 0 <= n - 2 < n_steps:
+                e_out(*steps[n - 2])
             if n < n_steps:
-                b, h, t = steps[n]
-                b2, h2 = (b, h + 1) if h + 1 < H else (b + 1, 0)
-                if h == 0 and t == 0 and b + 1 < B:
-                    load(b + 1)
-                if b2 < B and t == 0:
-                    k_prep(b2, h2)
-                if b2 < B and t == 1:
-                    q_prep(b2, h2)
-                if b + 1 < B and t >= 2:
-                    item = 2 * h + (t - 2)
-                    if item == 0:
-                        batch_tiles(b + 1)
-                    if item < 2:
-                        x_half(b + 1, item)
-                    if item == 1:
-                        pv_group(b + 1)
-                    if item == 2:
-                        x_quant(b + 1)
-                        v_quant(b + 1, 0)
-                    if 2 <= item < 6:
-                        v_new(b + 1, item - 2)
-                    if item == 6:
-                        v_quant(b + 1, 1)
+                if t == 2 and hi + 2 < len(heads):
+                    k_out(*heads[hi + 2])
+                if t == 0 and 2 <= hi + 1 < len(heads):
+                    q_out(*heads[hi + 1])
+                if b + 1 < B and h == 0 and t == 0:
+                    load_tiles(b + 1)
+                    load_xv(b + 1)
+                    load_qk(b + 1, 0, H)
+            for fn in outs:
+                fn()

@@ -33,7 +33,6 @@ def tile_flashattentionmodule_pa_t_kernel(tc, x, q, k_new, past_k, past_v, Wv, b
         work = ctx.enter_context(tc.tile_pool(name="work", bufs=3))
         small = ctx.enter_context(tc.tile_pool(name="small", bufs=6))
         psum = ctx.enter_context(tc.psum_pool(name="psum", bufs=1))
-        ctx.enter_context(tc.manual_schedule())
 
         st = {}
 

@@ -112,7 +112,7 @@ def tile_flashattentionmodule_pa_t_kernel(tc, x, q, k_new, past_k, past_v, Wv, b
 
         def words_out(tp, grp, half):
             g32 = grp[:].bitcast(F32).rearrange("p (o m u) -> p o m u", o=4, u=2)
-            nc.vector.tensor_copy(
+            nc.scalar.copy(
                 out=g32[:, 2 * half:2 * half + 2],
                 in_=tp[:].rearrange("p (o u m) -> p o m u", o=2, u=2),
             )
@@ -245,64 +245,59 @@ def tile_flashattentionmodule_pa_t_kernel(tc, x, q, k_new, past_k, past_v, Wv, b
             st[("eT", b, h, t)] = eT
 
         def e_out(b, h, t):
-            egrp = work.tile([P, T], BF16, name="egrp", align_bytes=64, bufs=4)
-            dst = egrp[:].bitcast(F32).rearrange("p (g m u) -> p g m u", g=2, u=2)
+            if t % 2 == 0:
+                st[("egrp", b, h, t // 2)] = work.tile([P, 2 * T], BF16, name="egrp", align_bytes=64, bufs=3)
+            egrp = st[("egrp", b, h, t // 2)]
+            dst = egrp[:, (t % 2) * T:(t % 2 + 1) * T].bitcast(F32).rearrange("p (g m u) -> p g m u", g=2, u=2)
             src = st[("eT", b, h, t)][:].rearrange("p (g u m) -> p g m u", g=2, u=2)
             if (h % 2, t) in E_ON_VECTOR:
                 nc.vector.tensor_copy(out=dst, in_=src)
             else:
                 nc.scalar.copy(out=dst, in_=src)
-            st[("egrp", b, h, t)] = egrp
 
         def e_quant(b, h, t):
-            ec = work.tile([P, 256], U32, name="ec", align_bytes=64, bufs=16)
-            es = work.tile([P, 256], U8, name="es", align_bytes=64, bufs=16)
-            nc.vector.quantize_mx(out=ec[:].bitcast(FP8X4), scales=es[:], in_=st[("egrp", b, h, t)][:])
-            st[("ec", b, h, t)] = ec
-            st[("es", b, h, t)] = es
+            if t % 2 == 0:
+                return
+            ec = work.tile([P, 512], U32, name="ec", align_bytes=64, bufs=8)
+            es = work.tile([P, 512], U8, name="es", align_bytes=64, bufs=8)
+            nc.vector.quantize_mx(out=ec[:].bitcast(FP8X4), scales=es[:], in_=st[("egrp", b, h, t // 2)][:])
+            st[("ec", b, h, t // 2)] = ec
+            st[("es", b, h, t // 2)] = es
 
-        def pv_pair(b, h, t0):
+        def pv_tiles(b, h, t0, nt):
             ops = psum.tile([P, 512], F32, name="ops")
             vc = st[("vcodes", b)]
             vs = st[("vscales", b)]
-            for t in (t0, t0 + 1):
-                ec = st[("ec", b, h, t)]
-                es = st[("es", b, h, t)]
+            for t in range(t0, t0 + nt):
+                ec = st[("ec", b, h, t // 2)]
+                es = st[("es", b, h, t // 2)]
                 for g in range(2):
                     c0 = (g * H + h) * P
+                    c1 = ((t % 2) * 2 + g) * P
                     nc.tensor.matmul_mx(
                         out=ops[:, (t - t0) * P:(t - t0 + 1) * P],
-                        lhsT=ec[:, g * P:(g + 1) * P].bitcast(FP8X4),
-                        lhsT_scale=es[:, g * P:(g + 1) * P],
+                        lhsT=ec[:, c1:c1 + P].bitcast(FP8X4),
+                        lhsT_scale=es[:, c1:c1 + P],
                         rhs=vc[:, c0:c0 + P].bitcast(FP8X4),
                         rhs_scale=vs[:, c0:c0 + P],
                         start=(g == 0), stop=(g == 1),
                     )
             return ops
 
-        def finish_pair(ops, b, h, t0):
-            rc = small.tile([P, 2], F32, name="rc")
-            nc.vector.reciprocal(out=rc[:], in_=st[("rs", b, h)][:, t0:t0 + 2])
-            if t0 == 0:
-                st[("o", b, h)] = work.tile([P, NT * P], F32, name="o_sb")
-            o_sb = st[("o", b, h)]
+        def finish_tiles(ops, b, h, t0, nt):
+            rc = small.tile([P, NT], F32, name="rc")
+            nc.vector.reciprocal(out=rc[:, 0:nt], in_=st[("rs", b, h)][:, t0:t0 + nt])
+            o_sb = work.tile([P, NT * P], F32, name="o_sb")
             nc.vector.tensor_tensor(
-                out=o_sb[:, t0 * P:(t0 + 2) * P].rearrange("p (t d) -> p t d", t=2),
-                in0=ops[:, 0:2 * P].rearrange("p (t d) -> p t d", t=2),
-                in1=rc[:].unsqueeze(2).to_broadcast([P, 2, P]),
+                out=o_sb[:, 0:nt * P].rearrange("p (t d) -> p t d", t=nt),
+                in0=ops[:, 0:nt * P].rearrange("p (t d) -> p t d", t=nt),
+                in1=rc[:, 0:nt].unsqueeze(2).to_broadcast([P, nt, P]),
                 op=ALU.mult,
             )
-            last = b == B - 1 and h == H - 1
-            if t0 == 2 and not last:
-                nc.sync.dma_start(
-                    out=out[b, :, h * P:(h + 1) * P].rearrange("(t p) d -> p t d", p=P),
-                    in_=o_sb[:].rearrange("p (t d) -> p t d", t=NT),
-                )
-            if last:
-                nc.sync.dma_start(
-                    out=out[b, t0 * P:(t0 + 2) * P, h * P:(h + 1) * P].rearrange("(t p) d -> p t d", p=P),
-                    in_=o_sb[:, t0 * P:(t0 + 2) * P].rearrange("p (t d) -> p t d", t=2),
-                )
+            nc.sync.dma_start(
+                out=out[b, t0 * P:(t0 + nt) * P, h * P:(h + 1) * P].rearrange("(t p) d -> p t d", p=P),
+                in_=o_sb[:, 0:nt * P].rearrange("p (t d) -> p t d", t=nt),
+            )
 
         heads = [(b, h) for b in range(B) for h in range(H)]
         steps = [(b, h, t) for (b, h) in heads for t in range(NT)]
@@ -319,10 +314,15 @@ def tile_flashattentionmodule_pa_t_kernel(tc, x, q, k_new, past_k, past_v, Wv, b
         jobs = [("w", 0, 0), ("w", 0, 1), ("x", 0, 0), ("x", 0, 1), ("bias", 0, 0)] + value_jobs(0)[2:]
         for b in range(B):
             nxt = value_jobs(b + 1) if b + 1 < B else []
-            for j in range(2 * H):
-                jobs.append(("pair", b, j))
-                if j in (0, 1, 3, 4, 5, 6) and nxt:
-                    jobs.append(nxt.pop(0))
+            for h in range(H):
+                if b == B - 1 and h == H - 1:
+                    jobs.append(("pv", b, (h, 0, 2)))
+                    jobs.append(("pv", b, (h, 2, 2)))
+                else:
+                    jobs.append(("pv", b, (h, 0, NT)))
+                for rep in range(2):
+                    if nxt:
+                        jobs.append(nxt.pop(0))
 
         def run_job(job, outs, late):
             kind, b, j = job
@@ -350,15 +350,15 @@ def tile_flashattentionmodule_pa_t_kernel(tc, x, q, k_new, past_k, past_v, Wv, b
                 outs.append(lambda: vnew_out(vn, b, j))
                 if j == H - 1:
                     late.append(lambda: v_quant(b, 1))
-            if kind == "pair":
-                ops = pv_pair(b, j // 2, 2 * (j % 2))
-                outs.append(lambda: finish_pair(ops, b, j // 2, 2 * (j % 2)))
+            if kind == "pv":
+                ops = pv_tiles(b, j[0], j[1], j[2])
+                outs.append(lambda: finish_tiles(ops, b, j[0], j[1], j[2]))
 
         def job_ready(job, n):
             kind, b, j = job
-            if kind != "pair":
+            if kind != "pv":
                 return True
-            return (b * 2 * H + j) * 2 + 1 + 4 <= n
+            return (b * H + j[0]) * NT + j[1] + j[2] - 1 + 4 <= n
 
         batch_tiles(0)
         k_pe(0, 0, "tr")

@@ -112,7 +112,7 @@ def tile_flashattentionmodule_pa_t_kernel(tc, x, q, k_new, past_k, past_v, Wv, b
 
         def words_out(tp, grp, half):
             g32 = grp[:].bitcast(F32).rearrange("p (o m u) -> p o m u", o=4, u=2)
-            nc.scalar.copy(
+            nc.vector.tensor_copy(
                 out=g32[:, 2 * half:2 * half + 2],
                 in_=tp[:].rearrange("p (o u m) -> p o m u", o=2, u=2),
             )
@@ -193,7 +193,7 @@ def tile_flashattentionmodule_pa_t_kernel(tc, x, q, k_new, past_k, past_v, Wv, b
                 )
             st[("qtp", b, h)] = qtp
 
-        def q_out(b, h, copy_fn=nc.scalar.copy):
+        def q_out(b, h, copy_fn=nc.vector.tensor_copy):
             qT = headp.tile([P, S], BF16, name="qT")
             copy_fn(out=qT[:], in_=st[("qtp", b, h)][:])
             st[("qT", b, h)] = qT

@@ -7,20 +7,22 @@ from concourse.masks import make_identity
 BF16 = mybir.dt.bfloat16
 F32 = mybir.dt.float32
 U32 = mybir.dt.uint32
+I32 = mybir.dt.int32
 U8 = mybir.dt.uint8
 FP8X4 = mybir.dt.float8_e4m3fn_x4
 ALU = mybir.AluOpType
 ACT = mybir.ActivationFunctionType
 
 P = 128
+HALF = 64
 B, S, D, H, HD = 8, 512, 512, 4, 128
 T = 2 * S
 NT = S // P
 SCALE = 1.0 / math.sqrt(HD)
 MASK = -1.0e30
 FLOPS = 2 * B * S * D * D + 2 * 2 * B * H * S * T * HD
-PSUM_BUFS = {"tr": 1, "ops": 1, "eT": 2}
-E_ON_VECTOR = ()
+E01_COLS = 3 * S
+QLAG = 3
 
 
 def tile_flashattentionmodule_pa_t_kernel(tc, x, q, k_new, past_k, past_v, Wv, bv, out):
@@ -28,11 +30,12 @@ def tile_flashattentionmodule_pa_t_kernel(tc, x, q, k_new, past_k, past_v, Wv, b
     with ExitStack() as ctx:
         consts = ctx.enter_context(tc.tile_pool(name="consts", bufs=1))
         loads = ctx.enter_context(tc.tile_pool(name="loads", bufs=2))
-        batchp = ctx.enter_context(tc.tile_pool(name="batchp", bufs=3))
+        batchp = ctx.enter_context(tc.tile_pool(name="batchp", bufs=2))
         headp = ctx.enter_context(tc.tile_pool(name="headp", bufs=2))
         work = ctx.enter_context(tc.tile_pool(name="work", bufs=3))
-        small = ctx.enter_context(tc.tile_pool(name="small", bufs=6))
+        small = ctx.enter_context(tc.tile_pool(name="small", bufs=8))
         psum = ctx.enter_context(tc.psum_pool(name="psum", bufs=1))
+        ctx.enter_context(tc.manual_schedule())
 
         st = {}
 
@@ -43,13 +46,13 @@ def tile_flashattentionmodule_pa_t_kernel(tc, x, q, k_new, past_k, past_v, Wv, b
                     in_=src[b, h0:h1].rearrange("h (a p) d -> p h a d", p=P),
                 )
 
-        def load_xv(b):
-            xv = st[("x", b)][:].rearrange("p (u e f) -> p u e f", u=2, e=2)
-            for u in range(2):
-                nc.sync.dma_start(
-                    out=xv[:, u],
-                    in_=x[b, 256 * u:256 * (u + 1), :].rearrange("(m e) f -> m e f", e=2),
-                )
+        def load_x(b):
+            nc.sync.dma_start(
+                out=st[("x", b)][:].rearrange("p (j f) -> p j f", j=4),
+                in_=x[b].rearrange("(m j) f -> m j f", j=4),
+            )
+
+        def load_pv(b):
             nc.sync.dma_start(
                 out=st[("pv", b)][:].rearrange("p (h u e d) -> p h u e d", h=H, u=2, e=2),
                 in_=past_v[b].rearrange("h (u m e) d -> m h u e d", u=2, e=2),
@@ -61,13 +64,14 @@ def tile_flashattentionmodule_pa_t_kernel(tc, x, q, k_new, past_k, past_v, Wv, b
 
         load_tiles(0)
         load_qk(0, 0, 1)
-        load_qk(0, 1, 2)
         w_sb = consts.tile([P, 4 * D], BF16, name="w_sb")
         nc.sync.dma_start(
             out=w_sb[:].rearrange("p (o f) -> p o f", o=4),
             in_=Wv.rearrange("(o p) f -> p o f", p=P),
         )
-        load_xv(0)
+        load_qk(0, 1, 2)
+        load_x(0)
+        load_pv(0)
         load_qk(0, 2, H)
         ident_bf = consts.tile([P, P], BF16, name="ident_bf")
         make_identity(nc, ident_bf[:])
@@ -77,29 +81,41 @@ def tile_flashattentionmodule_pa_t_kernel(tc, x, q, k_new, past_k, past_v, Wv, b
             out=mask_f[:], in_=mask_f[:], compare_op=ALU.is_ge, fill=MASK,
             base=0, pattern=[[-1, P]], channel_multiplier=1,
         )
-        mask_bf = consts.tile([P, P], BF16, name="mask_bf")
-        nc.vector.tensor_copy(out=mask_bf[:], in_=mask_f[:])
         ident_f = consts.tile([P, P], F32, name="ident_f")
         make_identity(nc, ident_f[:])
-        e_tiles = []
-        for t in range(NT):
-            e_t = consts.tile([P, T], BF16, name="e%d" % t)
-            if t < NT - 1:
-                nc.gpsimd.memset(e_t[:, S + (t + 1) * P:], 0.0)
-            e_tiles.append(e_t)
         bias_bf = consts.tile([P, D], BF16, name="bias_bf")
-        nc.gpsimd.memset(bias_bf[:], 0.0)
+        nc.vector.memset(bias_bf[:], 0.0)
         nc.sync.dma_start(out=bias_bf[0:1, :], in_=bv.rearrange("(o n) -> o n", o=1))
         ones_bf = consts.tile([P, P], BF16, name="ones_bf")
-        nc.gpsimd.memset(ones_bf[:], 1.0)
+        nc.vector.memset(ones_bf[:], 1.0)
+        e01 = consts.tile([P, E01_COLS], BF16, name="e01")
+        nc.vector.memset(e01[:, S + P:S + 2 * P], 0.0)
+        e2 = consts.tile([P, T], BF16, name="e2")
+        nc.vector.memset(e2[:, T - P:], 0.0)
+        e3 = consts.tile([P, T], BF16, name="e3")
+        mask_bf = consts.tile([P, P], BF16, name="mask_bf")
+        nc.vector.tensor_copy(out=mask_bf[:], in_=mask_f[:])
         bias_f = consts.tile([P, D], F32, name="bias_f")
         wgrp = consts.tile([P, 4 * D], BF16, name="wgrp", align_bytes=64)
         wcodes = consts.tile([P, D], U32, name="wcodes", align_bytes=64)
         wscales = consts.tile([P, D], U8, name="wscales", align_bytes=64)
+        vscales = []
+        for i in range(2):
+            vs_t = consts.tile([P, 2 * H * HD], U8, name="vscales%d" % i, align_bytes=64)
+            vscales.append(vs_t)
+        vlo = []
+        vhi = []
+        for i in range(2):
+            lo_c = consts.tile([P, H * HD], U32, name="lo_c%d" % i, align_bytes=64)
+            lo_s = consts.tile([P, H * HD], U8, name="lo_s%d" % i, align_bytes=64)
+            hi_c = consts.tile([P, H * HD], U32, name="hi_c%d" % i, align_bytes=64)
+            hi_s = consts.tile([P, H * HD], U8, name="hi_s%d" % i, align_bytes=64)
+            vlo.append((lo_c, lo_s))
+            vhi.append((hi_c, hi_s))
 
-        def words_pe(src, half):
+        def words_pe(src, half, tag, bufs):
             s32 = src[:].bitcast(F32)
-            tp = psum.tile([P, 512], F32, name="tp", tag="ops")
+            tp = psum.tile([P, 512], F32, name="tp", tag=tag, bufs=bufs)
             for oo in range(2):
                 for u in range(2):
                     o = 2 * half + oo
@@ -110,9 +126,9 @@ def tile_flashattentionmodule_pa_t_kernel(tc, x, q, k_new, past_k, past_v, Wv, b
                     )
             return tp
 
-        def words_out(tp, grp, half):
+        def words_out(tp, grp, half, copy_fn):
             g32 = grp[:].bitcast(F32).rearrange("p (o m u) -> p o m u", o=4, u=2)
-            nc.vector.tensor_copy(
+            copy_fn(
                 out=g32[:, 2 * half:2 * half + 2],
                 in_=tp[:].rearrange("p (o u m) -> p o m u", o=2, u=2),
             )
@@ -123,7 +139,6 @@ def tile_flashattentionmodule_pa_t_kernel(tc, x, q, k_new, past_k, past_v, Wv, b
             st[("xscales", b)] = batchp.tile([P, D], U8, name="xscales", align_bytes=64)
             st[("vgrp", b)] = batchp.tile([P, 2 * H * HD * 4], BF16, name="vgrp", align_bytes=64)
             st[("vcodes", b)] = batchp.tile([P, 2 * H * HD], U32, name="vcodes", align_bytes=64)
-            st[("vscales", b)] = batchp.tile([P, 2 * H * HD], U8, name="vscales", align_bytes=64)
 
         def x_quant(b):
             nc.vector.quantize_mx(
@@ -139,9 +154,18 @@ def tile_flashattentionmodule_pa_t_kernel(tc, x, q, k_new, past_k, past_v, Wv, b
         def v_quant(b, g):
             nc.vector.quantize_mx(
                 out=st[("vcodes", b)][:, g * 512:(g + 1) * 512].bitcast(FP8X4),
-                scales=st[("vscales", b)][:, g * 512:(g + 1) * 512],
+                scales=vscales[b % 2][:, g * 512:(g + 1) * 512],
                 in_=st[("vgrp", b)][:, g * 2048:(g + 1) * 2048],
             )
+
+        def v_move(b):
+            for p0, (c, s) in ((0, vlo[b % 2]), (HALF, vhi[b % 2])):
+                nc.sync.dma_start(
+                    out=c[p0:p0 + HALF, :].bitcast(I32), in_=st[("vcodes", b)][0:HALF, 512:1024].bitcast(I32)
+                )
+                nc.sync.dma_start(
+                    out=s[p0:p0 + HALF, :].bitcast(I32), in_=vscales[b % 2][0:HALF, 512:1024].bitcast(I32)
+                )
 
         def vnew_pe(b, h):
             vn = psum.tile([P, 512], F32, name="vn", tag="ops")
@@ -167,120 +191,141 @@ def tile_flashattentionmodule_pa_t_kernel(tc, x, q, k_new, past_k, past_v, Wv, b
                 op=ALU.add,
             )
 
-        def k_pe(b, h, tag="tr"):
-            ktp = psum.tile([P, T], BF16, name="ktp", tag=tag, bufs=PSUM_BUFS[tag])
-            for a in range(NT):
-                nc.tensor.transpose(
-                    ktp[:, a * P:(a + 1) * P], st[("pk", b)][:, (h * NT + a) * P:(h * NT + a + 1) * P], ident_bf[:]
-                )
-            for a in range(NT):
-                nc.tensor.transpose(
-                    ktp[:, S + a * P:S + (a + 1) * P], st[("kn", b)][:, (h * NT + a) * P:(h * NT + a + 1) * P],
-                    ident_bf[:],
-                )
+        def k_pe(b, h):
+            ktp = psum.tile([P, T], BF16, name="ktp", tag="tr")
+            for i, key in enumerate(("pk", "kn")):
+                for a in range(NT):
+                    nc.tensor.transpose(
+                        ktp[:, i * S + a * P:i * S + (a + 1) * P],
+                        st[(key, b)][:, (h * NT + a) * P:(h * NT + a + 1) * P], ident_bf[:],
+                    )
             st[("ktp", b, h)] = ktp
 
-        def k_out(b, h):
+        def k_out(b, h, copy_fn):
             kT = headp.tile([P, T], BF16, name="kT")
-            nc.scalar.copy(out=kT[:], in_=st[("ktp", b, h)][:])
+            copy_fn(out=kT[:], in_=st[("ktp", b, h)][:])
             st[("kT", b, h)] = kT
 
-        def q_pe(b, h, tag="tr"):
-            qtp = psum.tile([P, S], BF16, name="qtp", tag=tag, bufs=PSUM_BUFS[tag])
+        def q_pe(b, h, tag, bufs):
+            qtp = psum.tile([P, S], BF16, name="qtp", tag=tag, bufs=bufs)
             for a in range(NT):
                 nc.tensor.transpose(
                     qtp[:, a * P:(a + 1) * P], st[("q", b)][:, (h * NT + a) * P:(h * NT + a + 1) * P], ident_bf[:]
                 )
             st[("qtp", b, h)] = qtp
 
-        def q_out(b, h, copy_fn=nc.vector.tensor_copy):
+        def q_out(b, h, copy_fn):
             qT = headp.tile([P, S], BF16, name="qT")
             copy_fn(out=qT[:], in_=st[("qtp", b, h)][:])
             st[("qT", b, h)] = qT
             st[("rs", b, h)] = headp.tile([P, NT], F32, name="rs", bufs=8)
 
-        def scores(b, h, t):
+        def scores_past(b, h, t):
             sA = psum.tile([P, 512], F32, name="sA", bufs=2)
+            nc.tensor.matmul(
+                sA[:], lhsT=st[("qT", b, h)][:, t * P:(t + 1) * P], rhs=st[("kT", b, h)][:, 0:S], start=True, stop=True
+            )
+            st[("sA", b, h, t)] = sA
+
+        def scores_new(b, h, t):
             sB = psum.tile([P, 512], F32, name="sB", bufs=2)
             kT = st[("kT", b, h)]
             lq = st[("qT", b, h)][:, t * P:(t + 1) * P]
-            nc.tensor.matmul(sA[:], lhsT=lq, rhs=kT[:, 0:S], start=True, stop=True)
             if t > 0:
                 nc.tensor.matmul(sB[:, 0:t * P], lhsT=lq, rhs=kT[:, S:S + t * P], start=True, stop=True)
             nc.tensor.matmul(
                 sB[:, t * P:(t + 1) * P], lhsT=lq, rhs=kT[:, S + t * P:S + (t + 1) * P], start=True, stop=False
             )
             nc.tensor.matmul(sB[:, t * P:(t + 1) * P], lhsT=ident_bf[:], rhs=mask_bf[:], start=False, stop=True)
-            st[("sA", b, h, t)] = sA
             st[("sB", b, h, t)] = sB
 
-        def rowmax(b, h, t):
-            w = (t + 1) * P
-            sc = work.tile([P, T], F32, name="sc", bufs=4)
+        def rowmax_past(b, h, t):
+            sc = work.tile([P, T], F32, name="sc", bufs=6)
             a0 = small.tile([P, 1], F32, name="a0")
-            nb = small.tile([P, 1], F32, name="nb")
+            past0 = 2 * P if t == 1 else 0
             nc.vector.tensor_scalar(
-                out=sc[:, 0:S], in0=st[("sA", b, h, t)][:], scalar1=-SCALE, scalar2=None,
+                out=sc[:, past0:past0 + S], in0=st[("sA", b, h, t)][:], scalar1=-SCALE, scalar2=None,
                 op0=ALU.mult, op1=ALU.min, accum_out=a0[:],
             )
-            nc.vector.tensor_scalar(
-                out=sc[:, S:S + w], in0=st[("sB", b, h, t)][:, 0:w], scalar1=-SCALE, scalar2=a0[:],
-                op0=ALU.mult, op1=ALU.min, accum_out=nb[:],
-            )
             st[("sc", b, h, t)] = sc
+            st[("a0", b, h, t)] = a0
+
+        def rowmax_new(b, h, t):
+            w = (t + 1) * P
+            nb = small.tile([P, 1], F32, name="nb")
+            new0 = 0 if t == 1 else S
+            nc.vector.tensor_scalar(
+                out=st[("sc", b, h, t)][:, new0:new0 + w], in0=st[("sB", b, h, t)][:, 0:w], scalar1=-SCALE,
+                scalar2=st[("a0", b, h, t)][:], op0=ALU.mult, op1=ALU.min, accum_out=nb[:],
+            )
             st[("nb", b, h, t)] = nb
 
         def expo(b, h, t):
             w = S + (t + 1) * P
+            dst = (e01[:, 0:w], e01[:, S + 2 * P:E01_COLS], e2[:, 0:w], e3[:, 0:w])[t]
             nc.scalar.activation(
-                out=e_tiles[t][:, 0:w], in_=st[("sc", b, h, t)][:, 0:w], func=ACT.Exp,
+                out=dst, in_=st[("sc", b, h, t)][:, 0:w], func=ACT.Exp,
                 bias=st[("nb", b, h, t)][:], scale=-1.0, accum_out=st[("rs", b, h)][:, t:t + 1],
             )
 
+        def e_words(t):
+            w01 = e01[:].bitcast(F32)
+            if t == 0:
+                return [w01[:, u * P:(u + 1) * P] for u in range(2)]
+            if t == 1:
+                return [w01[:, 256 + u:512:2] for u in range(2)] + [w01[:, 512 + u * P:512 + (u + 1) * P] for u in range(2)]
+            w = (e2 if t == 2 else e3)[:].bitcast(F32)
+            return [w[:, u * P:(u + 1) * P] for u in range(2)] + [w[:, 256 + u:512:2] for u in range(2)]
+
         def e_pe(b, h, t):
             eT = psum.tile([P, 512], F32, name="eT", bufs=2)
-            e32 = e_tiles[t][:].bitcast(F32)
-            for j in range(4):
-                nc.tensor.transpose(eT[:, j * P:(j + 1) * P], e32[:, j * P:(j + 1) * P], ident_f[:])
+            for j, words in enumerate(e_words(t)):
+                nc.tensor.transpose(eT[:, j * P:(j + 1) * P], words, ident_f[:])
             st[("eT", b, h, t)] = eT
 
         def e_out(b, h, t):
             if t % 2 == 0:
                 st[("egrp", b, h, t // 2)] = work.tile([P, 2 * T], BF16, name="egrp", align_bytes=64, bufs=3)
             egrp = st[("egrp", b, h, t // 2)]
-            dst = egrp[:, (t % 2) * T:(t % 2 + 1) * T].bitcast(F32).rearrange("p (g m u) -> p g m u", g=2, u=2)
-            src = st[("eT", b, h, t)][:].rearrange("p (g u m) -> p g m u", g=2, u=2)
-            if (h % 2, t) in E_ON_VECTOR:
-                nc.vector.tensor_copy(out=dst, in_=src)
-            else:
-                nc.scalar.copy(out=dst, in_=src)
+            g0 = (0, 1, 0, 2)[t]
+            ng = (1, 2, 2, 2)[t]
+            nc.scalar.copy(
+                out=egrp[:, g0 * S:(g0 + ng) * S].bitcast(F32).rearrange("p (g m u) -> p g m u", g=ng, u=2),
+                in_=st[("eT", b, h, t)][:, 0:ng * 256].rearrange("p (g u m) -> p g m u", g=ng, u=2),
+            )
 
-        def e_quant(b, h, t):
-            if t % 2 == 0:
-                return
+        def e_quant(b, h, i):
             ec = work.tile([P, 512], U32, name="ec", align_bytes=64, bufs=8)
             es = work.tile([P, 512], U8, name="es", align_bytes=64, bufs=8)
-            nc.vector.quantize_mx(out=ec[:].bitcast(FP8X4), scales=es[:], in_=st[("egrp", b, h, t // 2)][:])
-            st[("ec", b, h, t // 2)] = ec
-            st[("es", b, h, t // 2)] = es
+            egrp = st[("egrp", b, h, i)]
+            for g0, ng in (((0, 2), (2, 1)), ((0, 4),))[i]:
+                nc.vector.quantize_mx(
+                    out=ec[:, g0 * P:(g0 + ng) * P].bitcast(FP8X4), scales=es[:, g0 * P:(g0 + ng) * P],
+                    in_=egrp[:, g0 * S:(g0 + ng) * S],
+                )
+            st[("ec", b, h, i)] = ec
+            st[("es", b, h, i)] = es
 
         def pv_tiles(b, h, t0, nt):
             ops = psum.tile([P, 512], F32, name="ops")
             vc = st[("vcodes", b)]
-            vs = st[("vscales", b)]
+            vs = vscales[b % 2]
+            past = (vc[:, h * P:(h + 1) * P], vs[:, h * P:(h + 1) * P])
+            new = (vc[:, (H + h) * P:(H + h + 1) * P], vs[:, (H + h) * P:(H + h + 1) * P])
+            lo = tuple(a[:, h * P:(h + 1) * P] for a in vlo[b % 2])
+            hi = tuple(a[:, h * P:(h + 1) * P] for a in vhi[b % 2])
+            plan = (((0, past), (1, lo)), ((2, past), (1, hi)), ((0, past), (1, new)), ((2, past), (3, new)))
             for t in range(t0, t0 + nt):
                 ec = st[("ec", b, h, t // 2)]
                 es = st[("es", b, h, t // 2)]
-                for g in range(2):
-                    c0 = (g * H + h) * P
-                    c1 = ((t % 2) * 2 + g) * P
+                for i, (c, (rc, rs)) in enumerate(plan[t]):
                     nc.tensor.matmul_mx(
                         out=ops[:, (t - t0) * P:(t - t0 + 1) * P],
-                        lhsT=ec[:, c1:c1 + P].bitcast(FP8X4),
-                        lhsT_scale=es[:, c1:c1 + P],
-                        rhs=vc[:, c0:c0 + P].bitcast(FP8X4),
-                        rhs_scale=vs[:, c0:c0 + P],
-                        start=(g == 0), stop=(g == 1),
+                        lhsT=ec[:, c * P:(c + 1) * P].bitcast(FP8X4),
+                        lhsT_scale=es[:, c * P:(c + 1) * P],
+                        rhs=rc.bitcast(FP8X4),
+                        rhs_scale=rs,
+                        start=(i == 0), stop=(i == 1),
                     )
             return ops
 
@@ -311,7 +356,7 @@ def tile_flashattentionmodule_pa_t_kernel(tc, x, q, k_new, past_k, past_v, Wv, b
         def value_jobs(b):
             return [("x", b, 0), ("x", b, 1), ("vn", b, 0), ("vn", b, 1), ("vn", b, 2), ("vn", b, 3)]
 
-        jobs = [("w", 0, 0), ("w", 0, 1), ("x", 0, 0), ("x", 0, 1), ("bias", 0, 0)] + value_jobs(0)[2:]
+        jobs = [("x", 0, 0), ("x", 0, 1), ("bias", 0, 0)] + value_jobs(0)[2:] + [("none", 0, 0)] * 4
         for b in range(B):
             nxt = value_jobs(b + 1) if b + 1 < B else []
             for h in range(H):
@@ -324,24 +369,22 @@ def tile_flashattentionmodule_pa_t_kernel(tc, x, q, k_new, past_k, past_v, Wv, b
                     if nxt:
                         jobs.append(nxt.pop(0))
 
-        def run_job(job, outs, late):
+        def job_transposes(job, sout, late):
             kind, b, j = job
-            if kind == "w":
-                tp = words_pe(w_sb, j)
-                outs.append(lambda: words_out(tp, wgrp, j))
-                if j == 1:
-                    late.append(lambda: nc.vector.quantize_mx(
-                        out=wcodes[:].bitcast(FP8X4), scales=wscales[:], in_=wgrp[:]))
             if kind == "x":
                 if j == 0 and b > 0:
                     batch_tiles(b)
                     for h in range(H):
                         pv_group(b, h)
-                tp = words_pe(st[("x", b)], j)
-                outs.append(lambda: words_out(tp, st[("xgrp", b)], j))
+                tp = words_pe(st[("x", b)], j, "ops", 1)
+                sout.append(lambda: words_out(tp, st[("xgrp", b)], j, nc.scalar.copy))
                 if j == 1:
+                    late.append(lambda: None)
                     late.append(lambda: x_quant(b))
                     late.append(lambda: v_quant(b, 0))
+
+        def job_matmuls(job, outs, late):
+            kind, b, j = job
             if kind == "bias":
                 bp = bias_pe()
                 outs.append(lambda: nc.vector.tensor_copy(out=bias_f[:], in_=bp[:]))
@@ -350,6 +393,7 @@ def tile_flashattentionmodule_pa_t_kernel(tc, x, q, k_new, past_k, past_v, Wv, b
                 outs.append(lambda: vnew_out(vn, b, j))
                 if j == H - 1:
                     late.append(lambda: v_quant(b, 1))
+                    late.append(lambda: v_move(b))
             if kind == "pv":
                 ops = pv_tiles(b, j[0], j[1], j[2])
                 outs.append(lambda: finish_tiles(ops, b, j[0], j[1], j[2]))
@@ -358,61 +402,93 @@ def tile_flashattentionmodule_pa_t_kernel(tc, x, q, k_new, past_k, past_v, Wv, b
             kind, b, j = job
             if kind != "pv":
                 return True
-            return (b * H + j[0]) * NT + j[1] + j[2] - 1 + 4 <= n
+            return (b * H + j[0]) * NT + j[1] + j[2] - 1 + QLAG <= n
 
         batch_tiles(0)
-        k_pe(0, 0, "tr")
-        q_pe(0, 0, "ops")
-        k_out(0, 0)
+        k_pe(0, 0)
+        q_pe(0, 0, "ops", 1)
+        k_out(0, 0, nc.scalar.copy)
         q_out(0, 0, nc.vector.tensor_copy)
-        k_pe(0, 1, "eT")
-        q_pe(0, 1, "eT")
-        k_out(0, 1)
-        q_out(0, 1, nc.vector.tensor_copy)
         for n in range(2):
-            scores(*steps[n])
-            rowmax(*steps[n])
+            scores_past(*steps[n])
+            scores_new(*steps[n])
+        rowmax_past(*steps[0])
+        k_pe(0, 1)
+        q_pe(0, 1, "ops", 1)
+        rowmax_past(*steps[1])
+        rowmax_new(*steps[0])
+        k_out(0, 1, nc.scalar.copy)
+        q_out(0, 1, nc.vector.tensor_copy)
+        scores_past(*steps[2])
+        rowmax_past(*steps[2])
+        rowmax_new(*steps[1])
+        wt = [words_pe(w_sb, j, "eT", 2) for j in range(2)]
+        for j in range(2):
+            words_out(wt[j], wgrp, j, nc.vector.tensor_copy)
+        scores_new(*steps[2])
+        scores_past(*steps[3])
         for h in range(H):
             pv_group(0, h)
+        for i in range(2):
+            nc.gpsimd.memset(vscales[i][:].bitcast(U32), 0)
+            for c, s in (vlo[i], vhi[i]):
+                nc.gpsimd.memset(c[:], 0)
+                nc.gpsimd.memset(s[:].bitcast(U32), 0)
 
-        late = []
-        for n in range(n_steps + 4 + 40):
-            if n >= n_steps + 3 and not jobs and not late:
+        outs = []
+        sout = []
+        late = [lambda: nc.vector.quantize_mx(out=wcodes[:].bitcast(FP8X4), scales=wscales[:], in_=wgrp[:])]
+        q_wait = []
+        for n in range(n_steps + 40):
+            if n > n_steps and not jobs and not outs and not late:
                 break
-            now = late
-            late = []
-            outs = []
             b, h, t = steps[min(n, n_steps - 1)]
             hi = heads.index((b, h))
-            for fn in now:
-                fn()
-            if 0 <= n - 3 < n_steps:
-                e_quant(*steps[n - 3])
-            for part in ("A", "D", "J", "K"):
-                if part == "A" and n + 2 < n_steps:
-                    scores(*steps[n + 2])
-                    rowmax(*steps[n + 2])
-                if part == "D" and 0 <= n - 1 < n_steps:
-                    e_pe(*steps[n - 1])
-                if part == "J" and jobs and job_ready(jobs[0], n):
-                    run_job(jobs.pop(0), outs, late)
-                if part == "K" and n < n_steps and hi + 2 < len(heads):
-                    if t == 1:
-                        k_pe(*heads[hi + 2])
-                    if t == 3:
-                        q_pe(*heads[hi + 2])
-            if n < n_steps:
-                expo(*steps[n])
-            if 0 <= n - 2 < n_steps:
-                e_out(*steps[n - 2])
-            if n < n_steps:
-                if t == 2 and hi + 2 < len(heads):
-                    k_out(*heads[hi + 2])
-                if t == 0 and 2 <= hi + 1 < len(heads):
-                    q_out(*heads[hi + 1])
-                if b + 1 < B and h == 0 and t == 0:
-                    load_tiles(b + 1)
-                    load_xv(b + 1)
-                    load_qk(b + 1, 0, H)
+            if 1 <= n - QLAG < n_steps and steps[n - QLAG][2] % 2 == 1:
+                b2, h2, t2 = steps[n - QLAG]
+                e_quant(b2, h2, t2 // 2)
             for fn in outs:
                 fn()
+            outs = []
+            if late:
+                late.pop(0)()
+            for fn in sout:
+                fn()
+            sout = []
+            for hd in q_wait:
+                q_out(*hd, nc.scalar.copy)
+            q_wait = []
+            if 0 <= n - 1 < n_steps:
+                e_pe(*steps[n - 1])
+            job = ("none", 0, 0)
+            if jobs and job_ready(jobs[0], n):
+                job = jobs.pop(0)
+            job_transposes(job, sout, late)
+            if n < n_steps and hi + 2 < len(heads):
+                if t == 1:
+                    k_pe(*heads[hi + 2])
+                if t == 2:
+                    q_pe(*heads[hi + 2], "tr", 1)
+            if n + 4 < n_steps:
+                scores_past(*steps[n + 4])
+            job_matmuls(job, outs, late)
+            if n + 3 < n_steps:
+                scores_new(*steps[n + 3])
+            if n < n_steps:
+                expo(*steps[n])
+            if 0 <= n - 1 < n_steps:
+                e_out(*steps[n - 1])
+            if n < n_steps and hi + 2 < len(heads):
+                if t == 1:
+                    k_out(*heads[hi + 2], nc.scalar.copy)
+                if t == 2:
+                    q_wait.append(heads[hi + 2])
+            if n + 3 < n_steps:
+                rowmax_past(*steps[n + 3])
+            if n + 2 < n_steps:
+                rowmax_new(*steps[n + 2])
+            if n < n_steps and b + 1 < B and h == 0 and t == 0:
+                load_tiles(b + 1)
+                load_x(b + 1)
+                load_pv(b + 1)
+                load_qk(b + 1, 0, H)

@@ -23,6 +23,7 @@ MASK = -1.0e30
 FLOPS = 2 * B * S * D * D + 2 * 2 * B * H * S * T * HD
 E01_COLS = 3 * S
 QLAG = 3
+LOAD_STEPS = ((3, 6, 8), (12, 4, 8))
 
 
 def tile_flashattentionmodule_pa_t_kernel(tc, x, q, k_new, past_k, past_v, Wv, bv, out):
@@ -58,21 +59,22 @@ def tile_flashattentionmodule_pa_t_kernel(tc, x, q, k_new, past_k, past_v, Wv, b
                 in_=past_v[b].rearrange("h (u m e) d -> m h u e d", u=2, e=2),
             )
 
-        def load_tiles(b):
-            for key in ("x", "pv", "pk", "kn", "q"):
+        def load_tiles(b, keys):
+            for key in keys:
                 st[(key, b)] = loads.tile([P, H * S], BF16, name=key + "_sb")
 
-        load_tiles(0)
+        load_tiles(0, ("x", "pv", "pk", "kn", "q"))
         load_qk(0, 0, 1)
+        load_qk(0, 1, 2)
         w_sb = consts.tile([P, 4 * D], BF16, name="w_sb")
         nc.sync.dma_start(
             out=w_sb[:].rearrange("p (o f) -> p o f", o=4),
             in_=Wv.rearrange("(o p) f -> p o f", p=P),
         )
-        load_qk(0, 1, 2)
         load_x(0)
+        load_qk(0, 2, 3)
         load_pv(0)
-        load_qk(0, 2, H)
+        load_qk(0, 3, H)
         ident_bf = consts.tile([P, P], BF16, name="ident_bf")
         make_identity(nc, ident_bf[:])
         mask_f = consts.tile([P, P], F32, name="mask_f")
@@ -487,8 +489,15 @@ def tile_flashattentionmodule_pa_t_kernel(tc, x, q, k_new, past_k, past_v, Wv, b
                 rowmax_past(*steps[n + 3])
             if n + 2 < n_steps:
                 rowmax_new(*steps[n + 2])
-            if n < n_steps and b + 1 < B and h == 0 and t == 0:
-                load_tiles(b + 1)
-                load_x(b + 1)
-                load_pv(b + 1)
-                load_qk(b + 1, 0, H)
+            for c, s in ((1, n), (b + 2, 4 * h + t)):
+                if c >= B or n >= n_steps:
+                    continue
+                if s == LOAD_STEPS[c > 1][0]:
+                    load_tiles(c, ("pk", "kn", "q"))
+                    load_qk(c, 0, H)
+                if s == LOAD_STEPS[c > 1][1]:
+                    load_tiles(c, ("x",))
+                    load_x(c)
+                if s == LOAD_STEPS[c > 1][2]:
+                    load_tiles(c, ("pv",))
+                    load_pv(c)

@@ -23,6 +23,7 @@ MASK = -1.0e30
 FLOPS = 2 * B * S * D * D + 2 * 2 * B * H * S * T * HD
 E01_COLS = 3 * S
 QLAG = 3
+JOB_BANK = (None, "ops", "tr", "ops")
 LOAD_STEPS = ((3, 6, 8), (12, 4, 8))
 
 
@@ -97,6 +98,8 @@ def tile_flashattentionmodule_pa_t_kernel(tc, x, q, k_new, past_k, past_v, Wv, b
         e3 = consts.tile([P, T], BF16, name="e3")
         mask_bf = consts.tile([P, P], BF16, name="mask_bf")
         nc.vector.tensor_copy(out=mask_bf[:], in_=mask_f[:])
+        minus_one = consts.tile([P, NT], F32, name="minus_one")
+        nc.vector.memset(minus_one[:], -1.0)
         bias_f = consts.tile([P, D], F32, name="bias_f")
         wgrp = consts.tile([P, 4 * D], BF16, name="wgrp", align_bytes=64)
         wcodes = consts.tile([P, D], U32, name="wcodes", align_bytes=64)
@@ -169,8 +172,8 @@ def tile_flashattentionmodule_pa_t_kernel(tc, x, q, k_new, past_k, past_v, Wv, b
                     out=s[p0:p0 + HALF, :].bitcast(I32), in_=vscales[b % 2][0:HALF, 512:1024].bitcast(I32)
                 )
 
-        def vnew_pe(b, h):
-            vn = psum.tile([P, 512], F32, name="vn", tag="ops")
+        def vnew_pe(b, h, tag):
+            vn = psum.tile([P, 512], F32, name="vn", tag=tag)
             xc = st[("xcodes", b)]
             xs = st[("xscales", b)]
             for tau in range(4):
@@ -204,7 +207,7 @@ def tile_flashattentionmodule_pa_t_kernel(tc, x, q, k_new, past_k, past_v, Wv, b
             st[("ktp", b, h)] = ktp
 
         def k_out(b, h, copy_fn):
-            kT = headp.tile([P, T], BF16, name="kT")
+            kT = headp.tile([P, T], BF16, name="kT", bufs=3)
             copy_fn(out=kT[:], in_=st[("ktp", b, h)][:])
             st[("kT", b, h)] = kT
 
@@ -217,7 +220,7 @@ def tile_flashattentionmodule_pa_t_kernel(tc, x, q, k_new, past_k, past_v, Wv, b
             st[("qtp", b, h)] = qtp
 
         def q_out(b, h, copy_fn):
-            qT = headp.tile([P, S], BF16, name="qT")
+            qT = headp.tile([P, S], BF16, name="qT", bufs=3)
             copy_fn(out=qT[:], in_=st[("qtp", b, h)][:])
             st[("qT", b, h)] = qT
             st[("rs", b, h)] = headp.tile([P, NT], F32, name="rs", bufs=8)
@@ -285,13 +288,13 @@ def tile_flashattentionmodule_pa_t_kernel(tc, x, q, k_new, past_k, past_v, Wv, b
                 nc.tensor.transpose(eT[:, j * P:(j + 1) * P], words, ident_f[:])
             st[("eT", b, h, t)] = eT
 
-        def e_out(b, h, t):
+        def e_out(b, h, t, copy_fn):
             if t % 2 == 0:
                 st[("egrp", b, h, t // 2)] = work.tile([P, 2 * T], BF16, name="egrp", align_bytes=64, bufs=3)
             egrp = st[("egrp", b, h, t // 2)]
             g0 = (0, 1, 0, 2)[t]
             ng = (1, 2, 2, 2)[t]
-            nc.scalar.copy(
+            copy_fn(
                 out=egrp[:, g0 * S:(g0 + ng) * S].bitcast(F32).rearrange("p (g m u) -> p g m u", g=ng, u=2),
                 in_=st[("eT", b, h, t)][:, 0:ng * 256].rearrange("p (g u m) -> p g m u", g=ng, u=2),
             )
@@ -308,8 +311,8 @@ def tile_flashattentionmodule_pa_t_kernel(tc, x, q, k_new, past_k, past_v, Wv, b
             st[("ec", b, h, i)] = ec
             st[("es", b, h, i)] = es
 
-        def pv_tiles(b, h, t0, nt):
-            ops = psum.tile([P, 512], F32, name="ops")
+        def pv_tiles(b, h, t0, nt, tag):
+            ops = psum.tile([P, 512], F32, name="ops", tag=tag)
             vc = st[("vcodes", b)]
             vs = vscales[b % 2]
             past = (vc[:, h * P:(h + 1) * P], vs[:, h * P:(h + 1) * P])
@@ -333,7 +336,9 @@ def tile_flashattentionmodule_pa_t_kernel(tc, x, q, k_new, past_k, past_v, Wv, b
 
         def finish_tiles(ops, b, h, t0, nt):
             rc = small.tile([P, NT], F32, name="rc")
-            nc.vector.reciprocal(out=rc[:, 0:nt], in_=st[("rs", b, h)][:, t0:t0 + nt])
+            nc.gpsimd.tensor_tensor(
+                out=rc[:, 0:nt], in0=st[("rs", b, h)][:, t0:t0 + nt], in1=minus_one[:, 0:nt], op=ALU.pow
+            )
             o_sb = work.tile([P, NT * P], F32, name="o_sb")
             nc.vector.tensor_tensor(
                 out=o_sb[:, 0:nt * P].rearrange("p (t d) -> p t d", t=nt),
@@ -347,64 +352,68 @@ def tile_flashattentionmodule_pa_t_kernel(tc, x, q, k_new, past_k, past_v, Wv, b
             )
 
         heads = [(b, h) for b in range(B) for h in range(H)]
-        steps = [(b, h, t) for (b, h) in heads for t in range(NT)]
+        steps = [(b, h, t) for (b, h) in heads for t in ((2, 3, 0, 1) if (b, h) == heads[-1] else range(NT))]
         n_steps = len(steps)
+        quant_at = {(b, h, i): steps.index((b, h, 2 * i + 1)) + QLAG for (b, h) in heads for i in range(2)}
+        quant_at[(B - 1, H - 1, 0)] = n_steps + 1
 
-        def bias_pe():
-            bp = psum.tile([P, 512], F32, name="bp", tag="ops")
+        def bias_pe(tag):
+            bp = psum.tile([P, 512], F32, name="bp", tag=tag)
             nc.tensor.matmul(bp[:], lhsT=ones_bf[:], rhs=bias_bf[:], start=True, stop=True)
             return bp
 
-        def value_jobs(b):
-            return [("x", b, 0), ("x", b, 1), ("vn", b, 0), ("vn", b, 1), ("vn", b, 2), ("vn", b, 3)]
+        value_jobs = [("x", 0, 0), ("x", 0, 1), ("bias", 0, 0)] + [("vn", 0, h) for h in range(H)]
+        for b in range(1, B):
+            value_jobs += [("x", b, 0), ("x", b, 1)] + [("vn", b, h) for h in range(H)]
+        pv_jobs = [("pv", b, (h, 0, NT)) for (b, h) in heads[:-1]]
+        pv_jobs += [("pv", B - 1, (H - 1, 2, 2)), ("pv", B - 1, (H - 1, 0, 2))]
 
-        jobs = [("x", 0, 0), ("x", 0, 1), ("bias", 0, 0)] + value_jobs(0)[2:] + [("none", 0, 0)] * 4
-        for b in range(B):
-            nxt = value_jobs(b + 1) if b + 1 < B else []
-            for h in range(H):
-                if b == B - 1 and h == H - 1:
-                    jobs.append(("pv", b, (h, 0, 2)))
-                    jobs.append(("pv", b, (h, 2, 2)))
-                else:
-                    jobs.append(("pv", b, (h, 0, NT)))
-                for rep in range(2):
-                    if nxt:
-                        jobs.append(nxt.pop(0))
-
-        def job_transposes(job, sout, late):
+        def job_transposes(job, n, tag, sout, after):
             kind, b, j = job
             if kind == "x":
                 if j == 0 and b > 0:
                     batch_tiles(b)
                     for h in range(H):
                         pv_group(b, h)
-                tp = words_pe(st[("x", b)], j, "ops", 1)
+                tp = words_pe(st[("x", b)], j, tag, 1)
                 sout.append(lambda: words_out(tp, st[("xgrp", b)], j, nc.scalar.copy))
                 if j == 1:
-                    late.append(lambda: None)
-                    late.append(lambda: x_quant(b))
-                    late.append(lambda: v_quant(b, 0))
+                    after.setdefault(n + 2, []).append(lambda: x_quant(b))
+                    after.setdefault(n + 3, []).append(lambda: v_quant(b, 0))
+                    st[("ready", "vn", b)] = n + 3
 
-        def job_matmuls(job, outs, late):
+        def job_matmuls(job, n, tag, outs, sout, after):
             kind, b, j = job
             if kind == "bias":
-                bp = bias_pe()
-                outs.append(lambda: nc.vector.tensor_copy(out=bias_f[:], in_=bp[:]))
+                bp = bias_pe(tag)
+                sout.append(lambda: nc.scalar.copy(out=bias_f[:], in_=bp[:]))
             if kind == "vn":
-                vn = vnew_pe(b, j)
+                vn = vnew_pe(b, j, tag)
                 outs.append(lambda: vnew_out(vn, b, j))
                 if j == H - 1:
-                    late.append(lambda: v_quant(b, 1))
-                    late.append(lambda: v_move(b))
+                    after.setdefault(n + 2, []).append(lambda: v_quant(b, 1))
+                    after.setdefault(n + 2, []).append(lambda: v_move(b))
+                    st[("ready", "pv", b)] = n + 5
             if kind == "pv":
-                ops = pv_tiles(b, j[0], j[1], j[2])
+                ops = pv_tiles(b, j[0], j[1], j[2], tag)
                 outs.append(lambda: finish_tiles(ops, b, j[0], j[1], j[2]))
 
-        def job_ready(job, n):
-            kind, b, j = job
-            if kind != "pv":
-                return True
-            return (b * H + j[0]) * NT + j[1] + j[2] - 1 + QLAG <= n
+        def next_job(n, t):
+            pv_ready = False
+            if pv_jobs:
+                kind, b, j = pv_jobs[0]
+                pv_ready = (
+                    st.get(("ready", "pv", b), n_steps) <= n
+                    and quant_at[(b, j[0], (j[1] + j[2] - 1) // 2)] + (n < n_steps) <= n
+                )
+            value_ready = bool(value_jobs) and pv_jobs[0][1] >= value_jobs[0][1] - 1
+            if value_ready and value_jobs[0][0] == "vn":
+                value_ready = st[("ready", "vn", value_jobs[0][1])] <= n
+            if pv_ready and (t == 3 or not value_ready):
+                return pv_jobs.pop(0)
+            if value_ready:
+                return value_jobs.pop(0)
+            return ("none", 0, 0)
 
         batch_tiles(0)
         k_pe(0, 0)
@@ -426,7 +435,7 @@ def tile_flashattentionmodule_pa_t_kernel(tc, x, q, k_new, past_k, past_v, Wv, b
         rowmax_new(*steps[1])
         wt = [words_pe(w_sb, j, "eT", 2) for j in range(2)]
         for j in range(2):
-            words_out(wt[j], wgrp, j, nc.vector.tensor_copy)
+            words_out(wt[j], wgrp, j, nc.scalar.copy)
         scores_new(*steps[2])
         scores_past(*steps[3])
         for h in range(H):
@@ -439,56 +448,53 @@ def tile_flashattentionmodule_pa_t_kernel(tc, x, q, k_new, past_k, past_v, Wv, b
 
         outs = []
         sout = []
-        late = [lambda: nc.vector.quantize_mx(out=wcodes[:].bitcast(FP8X4), scales=wscales[:], in_=wgrp[:])]
+        after = {0: [lambda: nc.vector.quantize_mx(out=wcodes[:].bitcast(FP8X4), scales=wscales[:], in_=wgrp[:])]}
         q_wait = []
         for n in range(n_steps + 40):
-            if n > n_steps and not jobs and not outs and not late:
+            if n > n_steps and not pv_jobs and not outs:
                 break
             b, h, t = steps[min(n, n_steps - 1)]
             hi = heads.index((b, h))
-            if 1 <= n - QLAG < n_steps and steps[n - QLAG][2] % 2 == 1:
-                b2, h2, t2 = steps[n - QLAG]
-                e_quant(b2, h2, t2 // 2)
-            for fn in outs:
-                fn()
-            outs = []
-            if late:
-                late.pop(0)()
-            for fn in sout:
-                fn()
-            sout = []
+            t = n % NT
+            for pair in [p for p in quant_at if quant_at[p] == n]:
+                e_quant(*pair)
             for hd in q_wait:
                 q_out(*hd, nc.scalar.copy)
             q_wait = []
+            now, outs = outs, []
+            snow, sout = sout, []
             if 0 <= n - 1 < n_steps:
                 e_pe(*steps[n - 1])
-            job = ("none", 0, 0)
-            if jobs and job_ready(jobs[0], n):
-                job = jobs.pop(0)
-            job_transposes(job, sout, late)
             if n < n_steps and hi + 2 < len(heads):
-                if t == 1:
+                if t == 0:
                     k_pe(*heads[hi + 2])
-                if t == 2:
+                if t == 1:
                     q_pe(*heads[hi + 2], "tr", 1)
+                    q_wait.append(heads[hi + 2])
+            tag = JOB_BANK[t] if n < n_steps else "ops"
+            job = next_job(n, t) if tag else ("none", 0, 0)
+            job_transposes(job, n, tag, sout, after)
             if n + 4 < n_steps:
                 scores_past(*steps[n + 4])
-            job_matmuls(job, outs, late)
+            job_matmuls(job, n, tag, outs, sout, after)
             if n + 3 < n_steps:
                 scores_new(*steps[n + 3])
             if n < n_steps:
                 expo(*steps[n])
             if 0 <= n - 1 < n_steps:
-                e_out(*steps[n - 1])
-            if n < n_steps and hi + 2 < len(heads):
-                if t == 1:
-                    k_out(*heads[hi + 2], nc.scalar.copy)
-                if t == 2:
-                    q_wait.append(heads[hi + 2])
+                e_out(*steps[n - 1], nc.vector.tensor_copy if n_steps - 3 <= n - 1 < n_steps - 1 else nc.scalar.copy)
+            if n < n_steps and hi + 2 < len(heads) and t == 0:
+                k_out(*heads[hi + 2], nc.scalar.copy)
+            for fn in snow:
+                fn()
             if n + 3 < n_steps:
                 rowmax_past(*steps[n + 3])
             if n + 2 < n_steps:
                 rowmax_new(*steps[n + 2])
+            for fn in now:
+                fn()
+            for fn in after.pop(n, []):
+                fn()
             for c, s in ((1, n), (b + 2, 4 * h + t)):
                 if c >= B or n >= n_steps:
                     continue

@@ -23,6 +23,7 @@ MASK = -1.0e30
 FLOPS = 2 * B * S * D * D + 2 * 2 * B * H * S * T * HD
 E01_COLS = 3 * S
 QLAG = 3
+FINISH_ON_SCALAR = (1,)
 JOB_BANK = (None, "ops", "tr", "ops")
 LOAD_STEPS = ((3, 6, 8), (12, 4, 8))
 
@@ -42,7 +43,7 @@ def tile_flashattentionmodule_pa_t_kernel(tc, x, q, k_new, past_k, past_v, Wv, b
         st = {}
 
         def load_qk(b, h0, h1):
-            for key, src in (("pk", past_k), ("kn", k_new), ("q", q)):
+            for key, src in (("q", q), ("pk", past_k), ("kn", k_new)):
                 nc.sync.dma_start(
                     out=st[(key, b)][:, h0 * S:h1 * S].rearrange("p (h a d) -> p h a d", h=h1 - h0, a=NT),
                     in_=src[b, h0:h1].rearrange("h (a p) d -> p h a d", p=P),
@@ -86,11 +87,11 @@ def tile_flashattentionmodule_pa_t_kernel(tc, x, q, k_new, past_k, past_v, Wv, b
         )
         ident_f = consts.tile([P, P], F32, name="ident_f")
         make_identity(nc, ident_f[:])
+        ones_bf = consts.tile([P, P], BF16, name="ones_bf")
+        nc.vector.memset(ones_bf[:], 1.0)
         bias_bf = consts.tile([P, D], BF16, name="bias_bf")
         nc.vector.memset(bias_bf[:], 0.0)
         nc.sync.dma_start(out=bias_bf[0:1, :], in_=bv.rearrange("(o n) -> o n", o=1))
-        ones_bf = consts.tile([P, P], BF16, name="ones_bf")
-        nc.vector.memset(ones_bf[:], 1.0)
         e01 = consts.tile([P, E01_COLS], BF16, name="e01")
         nc.vector.memset(e01[:, S + P:S + 2 * P], 0.0)
         e2 = consts.tile([P, T], BF16, name="e2")
@@ -196,27 +197,27 @@ def tile_flashattentionmodule_pa_t_kernel(tc, x, q, k_new, past_k, past_v, Wv, b
                 op=ALU.add,
             )
 
+        def half_pe(key, b, h, ktp, c0):
+            for a in range(NT):
+                nc.tensor.transpose(
+                    ktp[:, c0 + a * P:c0 + (a + 1) * P], st[(key, b)][:, (h * NT + a) * P:(h * NT + a + 1) * P],
+                    ident_bf[:],
+                )
+
         def k_pe(b, h):
             ktp = psum.tile([P, T], BF16, name="ktp", tag="tr")
-            for i, key in enumerate(("pk", "kn")):
-                for a in range(NT):
-                    nc.tensor.transpose(
-                        ktp[:, i * S + a * P:i * S + (a + 1) * P],
-                        st[(key, b)][:, (h * NT + a) * P:(h * NT + a + 1) * P], ident_bf[:],
-                    )
+            half_pe("pk", b, h, ktp, 0)
+            half_pe("kn", b, h, ktp, S)
             st[("ktp", b, h)] = ktp
 
-        def k_out(b, h, copy_fn):
+        def k_out(b, h):
             kT = headp.tile([P, T], BF16, name="kT", bufs=3)
-            copy_fn(out=kT[:], in_=st[("ktp", b, h)][:])
+            nc.scalar.copy(out=kT[:], in_=st[("ktp", b, h)][:])
             st[("kT", b, h)] = kT
 
         def q_pe(b, h, tag, bufs):
             qtp = psum.tile([P, S], BF16, name="qtp", tag=tag, bufs=bufs)
-            for a in range(NT):
-                nc.tensor.transpose(
-                    qtp[:, a * P:(a + 1) * P], st[("q", b)][:, (h * NT + a) * P:(h * NT + a + 1) * P], ident_bf[:]
-                )
+            half_pe("q", b, h, qtp, 0)
             st[("qtp", b, h)] = qtp
 
         def q_out(b, h, copy_fn):
@@ -334,18 +335,25 @@ def tile_flashattentionmodule_pa_t_kernel(tc, x, q, k_new, past_k, past_v, Wv, b
                     )
             return ops
 
-        def finish_tiles(ops, b, h, t0, nt):
+        def finish_tiles(ops, b, h, t0, nt, on_scalar):
             rc = small.tile([P, NT], F32, name="rc")
             nc.gpsimd.tensor_tensor(
                 out=rc[:, 0:nt], in0=st[("rs", b, h)][:, t0:t0 + nt], in1=minus_one[:, 0:nt], op=ALU.pow
             )
             o_sb = work.tile([P, NT * P], F32, name="o_sb")
-            nc.vector.tensor_tensor(
-                out=o_sb[:, 0:nt * P].rearrange("p (t d) -> p t d", t=nt),
-                in0=ops[:, 0:nt * P].rearrange("p (t d) -> p t d", t=nt),
-                in1=rc[:, 0:nt].unsqueeze(2).to_broadcast([P, nt, P]),
-                op=ALU.mult,
-            )
+            if on_scalar:
+                for i in range(nt):
+                    nc.scalar.activation(
+                        out=o_sb[:, i * P:(i + 1) * P], in_=ops[:, i * P:(i + 1) * P], func=ACT.Copy,
+                        scale=rc[:, i:i + 1],
+                    )
+            else:
+                nc.vector.tensor_tensor(
+                    out=o_sb[:, 0:nt * P].rearrange("p (t d) -> p t d", t=nt),
+                    in0=ops[:, 0:nt * P].rearrange("p (t d) -> p t d", t=nt),
+                    in1=rc[:, 0:nt].unsqueeze(2).to_broadcast([P, nt, P]),
+                    op=ALU.mult,
+                )
             nc.sync.dma_start(
                 out=out[b, t0 * P:(t0 + nt) * P, h * P:(h + 1) * P].rearrange("(t p) d -> p t d", p=P),
                 in_=o_sb[:, 0:nt * P].rearrange("p (t d) -> p t d", t=nt),
@@ -355,7 +363,13 @@ def tile_flashattentionmodule_pa_t_kernel(tc, x, q, k_new, past_k, past_v, Wv, b
         steps = [(b, h, t) for (b, h) in heads for t in ((2, 3, 0, 1) if (b, h) == heads[-1] else range(NT))]
         n_steps = len(steps)
         quant_at = {(b, h, i): steps.index((b, h, 2 * i + 1)) + QLAG for (b, h) in heads for i in range(2)}
+        late_e = range(n_steps - 4, n_steps - 1)
         quant_at[(B - 1, H - 1, 0)] = n_steps + 1
+
+        def warm(count):
+            junk = psum.tile([P, 512], F32, name="junk", tag="sA", bufs=2)
+            for i in range(count):
+                nc.tensor.matmul(junk[:, 0:P], lhsT=ones_bf[:], rhs=ones_bf[:], start=True, stop=True)
 
         def bias_pe(tag):
             bp = psum.tile([P, 512], F32, name="bp", tag=tag)
@@ -396,7 +410,8 @@ def tile_flashattentionmodule_pa_t_kernel(tc, x, q, k_new, past_k, past_v, Wv, b
                     st[("ready", "pv", b)] = n + 5
             if kind == "pv":
                 ops = pv_tiles(b, j[0], j[1], j[2], tag)
-                outs.append(lambda: finish_tiles(ops, b, j[0], j[1], j[2]))
+                on_scalar = j[0] in FINISH_ON_SCALAR and b < B - 1
+                (sout if on_scalar else outs).append(lambda: finish_tiles(ops, b, j[0], j[1], j[2], on_scalar))
 
         def next_job(n, t):
             pv_ready = False
@@ -416,27 +431,33 @@ def tile_flashattentionmodule_pa_t_kernel(tc, x, q, k_new, past_k, past_v, Wv, b
             return ("none", 0, 0)
 
         batch_tiles(0)
-        k_pe(0, 0)
+        warm(28)
         q_pe(0, 0, "ops", 1)
-        k_out(0, 0, nc.scalar.copy)
         q_out(0, 0, nc.vector.tensor_copy)
-        for n in range(2):
-            scores_past(*steps[n])
-            scores_new(*steps[n])
+        kT0 = headp.tile([P, T], BF16, name="kT", bufs=3)
+        st[("kT", 0, 0)] = kT0
+        for key, tag, bufs, c0 in (("pk", "tr", 1, 0), ("kn", "eT", 2, S)):
+            half = psum.tile([P, S], BF16, name="half", tag=tag, bufs=bufs)
+            half_pe(key, 0, 0, half, 0)
+            nc.scalar.copy(out=kT0[:, c0:c0 + S], in_=half[:])
+        scores_past(*steps[0])
         rowmax_past(*steps[0])
-        k_pe(0, 1)
-        q_pe(0, 1, "ops", 1)
+        scores_past(*steps[1])
         rowmax_past(*steps[1])
+        scores_new(*steps[0])
         rowmax_new(*steps[0])
-        k_out(0, 1, nc.scalar.copy)
+        scores_new(*steps[1])
+        q_pe(0, 1, "ops", 1)
         q_out(0, 1, nc.vector.tensor_copy)
+        k_pe(0, 1)
+        k_out(0, 1)
         scores_past(*steps[2])
         rowmax_past(*steps[2])
         rowmax_new(*steps[1])
+        scores_new(*steps[2])
         wt = [words_pe(w_sb, j, "eT", 2) for j in range(2)]
         for j in range(2):
             words_out(wt[j], wgrp, j, nc.scalar.copy)
-        scores_new(*steps[2])
         scores_past(*steps[3])
         for h in range(H):
             pv_group(0, h)
@@ -471,7 +492,9 @@ def tile_flashattentionmodule_pa_t_kernel(tc, x, q, k_new, past_k, past_v, Wv, b
                 if t == 1:
                     q_pe(*heads[hi + 2], "tr", 1)
                     q_wait.append(heads[hi + 2])
-            tag = JOB_BANK[t] if n < n_steps else "ops"
+            tag = JOB_BANK[t] if n < n_steps else ("tr", "ops")[n % 2]
+            if n == n_steps - 1:
+                tag = None
             job = next_job(n, t) if tag else ("none", 0, 0)
             job_transposes(job, n, tag, sout, after)
             if n + 4 < n_steps:
@@ -482,9 +505,9 @@ def tile_flashattentionmodule_pa_t_kernel(tc, x, q, k_new, past_k, past_v, Wv, b
             if n < n_steps:
                 expo(*steps[n])
             if 0 <= n - 1 < n_steps:
-                e_out(*steps[n - 1], nc.vector.tensor_copy if n_steps - 3 <= n - 1 < n_steps - 1 else nc.scalar.copy)
+                e_out(*steps[n - 1], nc.vector.tensor_copy if n - 1 in late_e else nc.scalar.copy)
             if n < n_steps and hi + 2 < len(heads) and t == 0:
-                k_out(*heads[hi + 2], nc.scalar.copy)
+                k_out(*heads[hi + 2])
             for fn in snow:
                 fn()
             if n + 3 < n_steps:

@@ -14,16 +14,16 @@ ALU = mybir.AluOpType
 ACT = mybir.ActivationFunctionType
 
 P = 128
-HALF = 64
 B, S, D, H, HD = 8, 512, 512, 4, 128
 T = 2 * S
 NT = S // P
 SCALE = 1.0 / math.sqrt(HD)
 MASK = -1.0e30
 FLOPS = 2 * B * S * D * D + 2 * 2 * B * H * S * T * HD
-E01_COLS = 3 * S
+E_COLS = 3 * S
+BLOCKS = 7
 QLAG = 3
-FINISH_ON_SCALAR = (1,)
+FINISH_ON_SCALAR = (0,)
 JOB_BANK = (None, "ops", "tr", "ops")
 LOAD_STEPS = ((3, 6, 8), (12, 4, 8))
 
@@ -92,10 +92,8 @@ def tile_flashattentionmodule_pa_t_kernel(tc, x, q, k_new, past_k, past_v, Wv, b
         bias_bf = consts.tile([P, D], BF16, name="bias_bf")
         nc.vector.memset(bias_bf[:], 0.0)
         nc.sync.dma_start(out=bias_bf[0:1, :], in_=bv.rearrange("(o n) -> o n", o=1))
-        e01 = consts.tile([P, E01_COLS], BF16, name="e01")
-        nc.vector.memset(e01[:, S + P:S + 2 * P], 0.0)
-        e2 = consts.tile([P, T], BF16, name="e2")
-        nc.vector.memset(e2[:, T - P:], 0.0)
+        e02 = consts.tile([P, E_COLS], BF16, name="e02")
+        e11 = consts.tile([P, E_COLS], BF16, name="e11")
         e3 = consts.tile([P, T], BF16, name="e3")
         mask_bf = consts.tile([P, P], BF16, name="mask_bf")
         nc.vector.tensor_copy(out=mask_bf[:], in_=mask_f[:])
@@ -109,15 +107,14 @@ def tile_flashattentionmodule_pa_t_kernel(tc, x, q, k_new, past_k, past_v, Wv, b
         for i in range(2):
             vs_t = consts.tile([P, 2 * H * HD], U8, name="vscales%d" % i, align_bytes=64)
             vscales.append(vs_t)
-        vlo = []
-        vhi = []
+        vsub = []
         for i in range(2):
-            lo_c = consts.tile([P, H * HD], U32, name="lo_c%d" % i, align_bytes=64)
-            lo_s = consts.tile([P, H * HD], U8, name="lo_s%d" % i, align_bytes=64)
-            hi_c = consts.tile([P, H * HD], U32, name="hi_c%d" % i, align_bytes=64)
-            hi_s = consts.tile([P, H * HD], U8, name="hi_s%d" % i, align_bytes=64)
-            vlo.append((lo_c, lo_s))
-            vhi.append((hi_c, hi_s))
+            sub = {}
+            for key in ("lo96", "hi32", "half"):
+                c = consts.tile([P, H * HD], U32, name="%s_c%d" % (key, i), align_bytes=64)
+                s = consts.tile([P, H * HD], U8, name="%s_s%d" % (key, i), align_bytes=64)
+                sub[key] = (c, s)
+            vsub.append(sub)
 
         def words_pe(src, half, tag, bufs):
             s32 = src[:].bitcast(F32)
@@ -165,13 +162,15 @@ def tile_flashattentionmodule_pa_t_kernel(tc, x, q, k_new, past_k, past_v, Wv, b
             )
 
         def v_move(b):
-            for p0, (c, s) in ((0, vlo[b % 2]), (HALF, vhi[b % 2])):
-                nc.sync.dma_start(
-                    out=c[p0:p0 + HALF, :].bitcast(I32), in_=st[("vcodes", b)][0:HALF, 512:1024].bitcast(I32)
-                )
-                nc.sync.dma_start(
-                    out=s[p0:p0 + HALF, :].bitcast(I32), in_=vscales[b % 2][0:HALF, 512:1024].bitcast(I32)
-                )
+            sub = vsub[b % 2]
+            for i, src in enumerate((st[("vcodes", b)], vscales[b % 2])):
+                new = src[:, 512:1024].bitcast(I32)
+                nc.sync.dma_start(out=sub["lo96"][i][0:96, :].bitcast(I32), in_=new[0:96, :])
+                nc.sync.dma_start(out=sub["hi32"][i][96:P, :].bitcast(I32), in_=new[0:32, :])
+                by_head = new.rearrange("p (g a d) -> p g a d", g=2, a=2)
+                half = sub["half"][i][:].bitcast(I32).rearrange("p (g a d) -> p g a d", g=2, a=2)
+                for a in range(2):
+                    nc.sync.dma_start(out=half[64 * a:64 * (a + 1), :, a], in_=by_head[0:64, :, a])
 
         def vnew_pe(b, h, tag):
             vn = psum.tile([P, 512], F32, name="vn", tag=tag)
@@ -245,10 +244,13 @@ def tile_flashattentionmodule_pa_t_kernel(tc, x, q, k_new, past_k, past_v, Wv, b
             nc.tensor.matmul(sB[:, t * P:(t + 1) * P], lhsT=ident_bf[:], rhs=mask_bf[:], start=False, stop=True)
             st[("sB", b, h, t)] = sB
 
+        def new_first(h, t):
+            return t == 0 or (t == 1 and h % 2 == 1)
+
         def rowmax_past(b, h, t):
             sc = work.tile([P, T], F32, name="sc", bufs=6)
             a0 = small.tile([P, 1], F32, name="a0")
-            past0 = 2 * P if t == 1 else 0
+            past0 = (t + 1) * P if new_first(h, t) else 0
             nc.vector.tensor_scalar(
                 out=sc[:, past0:past0 + S], in0=st[("sA", b, h, t)][:], scalar1=-SCALE, scalar2=None,
                 op0=ALU.mult, op1=ALU.min, accum_out=a0[:],
@@ -259,7 +261,7 @@ def tile_flashattentionmodule_pa_t_kernel(tc, x, q, k_new, past_k, past_v, Wv, b
         def rowmax_new(b, h, t):
             w = (t + 1) * P
             nb = small.tile([P, 1], F32, name="nb")
-            new0 = 0 if t == 1 else S
+            new0 = 0 if new_first(h, t) else S
             nc.vector.tensor_scalar(
                 out=st[("sc", b, h, t)][:, new0:new0 + w], in0=st[("sB", b, h, t)][:, 0:w], scalar1=-SCALE,
                 scalar2=st[("a0", b, h, t)][:], op0=ALU.mult, op1=ALU.min, accum_out=nb[:],
@@ -268,78 +270,97 @@ def tile_flashattentionmodule_pa_t_kernel(tc, x, q, k_new, past_k, past_v, Wv, b
 
         def expo(b, h, t):
             w = S + (t + 1) * P
-            dst = (e01[:, 0:w], e01[:, S + 2 * P:E01_COLS], e2[:, 0:w], e3[:, 0:w])[t]
+            tile = (e02, e11, e02, e3)[t]
+            c0 = E_COLS - w if new_first(h, t) else 0
             nc.scalar.activation(
-                out=dst, in_=st[("sc", b, h, t)][:, 0:w], func=ACT.Exp,
+                out=tile[:, c0:c0 + w], in_=st[("sc", b, h, t)][:, 0:w], func=ACT.Exp,
                 bias=st[("nb", b, h, t)][:], scale=-1.0, accum_out=st[("rs", b, h)][:, t:t + 1],
             )
 
-        def e_words(t):
-            w01 = e01[:].bitcast(F32)
-            if t == 0:
-                return [w01[:, u * P:(u + 1) * P] for u in range(2)]
-            if t == 1:
-                return [w01[:, 256 + u:512:2] for u in range(2)] + [w01[:, 512 + u * P:512 + (u + 1) * P] for u in range(2)]
-            w = (e2 if t == 2 else e3)[:].bitcast(F32)
-            return [w[:, u * P:(u + 1) * P] for u in range(2)] + [w[:, 256 + u:512:2] for u in range(2)]
+        def past_words(tile, c0):
+            w = tile[:].bitcast(F32)
+            return [w[:, c0 + u * P:c0 + (u + 1) * P] for u in range(2)]
+
+        def new_words(tile):
+            w = tile[:].bitcast(F32)
+            return [w[:, 256 + u:512:2] for u in range(2)]
+
+        def e_blocks(b, h, t):
+            done = order[(b, h)][:order[(b, h)].index(t)]
+            blocks = [("past", t, past_words((e02, e11, e02, e3)[t], 512 if new_first(h, t) else 0))]
+            if t == 3:
+                blocks.append(("new", 3, new_words(e3)))
+            if t in (0, 2) and 2 - t in done:
+                blocks.append(("new", 2, new_words(e02)))
+            if t == 1 and h % 2 == 1:
+                blocks.append(("new", 1, new_words(e11)))
+            return blocks
 
         def e_pe(b, h, t):
             eT = psum.tile([P, 512], F32, name="eT", bufs=2)
-            for j, words in enumerate(e_words(t)):
-                nc.tensor.transpose(eT[:, j * P:(j + 1) * P], words, ident_f[:])
+            j = 0
+            for kind, tt, words in e_blocks(b, h, t):
+                for w in words:
+                    nc.tensor.transpose(eT[:, j * P:(j + 1) * P], w, ident_f[:])
+                    j += 1
             st[("eT", b, h, t)] = eT
 
         def e_out(b, h, t, copy_fn):
-            if t % 2 == 0:
-                st[("egrp", b, h, t // 2)] = work.tile([P, 2 * T], BF16, name="egrp", align_bytes=64, bufs=3)
-            egrp = st[("egrp", b, h, t // 2)]
-            g0 = (0, 1, 0, 2)[t]
-            ng = (1, 2, 2, 2)[t]
+            if ("egrp", b, h) not in st:
+                st[("egrp", b, h)] = work.tile([P, BLOCKS * S], BF16, name="egrp", align_bytes=64, bufs=3)
+                st[("blocks", b, h)] = []
+            where = st[("blocks", b, h)]
+            g0 = len(where)
+            for kind, tt, words in e_blocks(b, h, t):
+                where.append((kind, tt))
+            ng = len(where) - g0
             copy_fn(
-                out=egrp[:, g0 * S:(g0 + ng) * S].bitcast(F32).rearrange("p (g m u) -> p g m u", g=ng, u=2),
+                out=st[("egrp", b, h)][:, g0 * S:(g0 + ng) * S].bitcast(F32).rearrange(
+                    "p (g m u) -> p g m u", g=ng, u=2),
                 in_=st[("eT", b, h, t)][:, 0:ng * 256].rearrange("p (g u m) -> p g m u", g=ng, u=2),
             )
 
-        def e_quant(b, h, i):
-            ec = work.tile([P, 512], U32, name="ec", align_bytes=64, bufs=8)
-            es = work.tile([P, 512], U8, name="es", align_bytes=64, bufs=8)
-            egrp = st[("egrp", b, h, i)]
-            for g0, ng in (((0, 2), (2, 1)), ((0, 4),))[i]:
-                nc.vector.quantize_mx(
-                    out=ec[:, g0 * P:(g0 + ng) * P].bitcast(FP8X4), scales=es[:, g0 * P:(g0 + ng) * P],
-                    in_=egrp[:, g0 * S:(g0 + ng) * S],
-                )
-            st[("ec", b, h, i)] = ec
-            st[("es", b, h, i)] = es
+        def e_quant(b, h, g0, ng):
+            if ("ec", b, h) not in st:
+                st[("ec", b, h)] = work.tile([P, BLOCKS * P], U32, name="ec", align_bytes=64, bufs=5)
+                st[("es", b, h)] = work.tile([P, BLOCKS * P], U8, name="es", align_bytes=64, bufs=5)
+            nc.vector.quantize_mx(
+                out=st[("ec", b, h)][:, g0 * P:(g0 + ng) * P].bitcast(FP8X4),
+                scales=st[("es", b, h)][:, g0 * P:(g0 + ng) * P],
+                in_=st[("egrp", b, h)][:, g0 * S:(g0 + ng) * S],
+            )
 
-        def pv_tiles(b, h, t0, nt, tag):
+        def pv_tiles(b, h, tiles, tag):
             ops = psum.tile([P, 512], F32, name="ops", tag=tag)
-            vc = st[("vcodes", b)]
-            vs = vscales[b % 2]
-            past = (vc[:, h * P:(h + 1) * P], vs[:, h * P:(h + 1) * P])
-            new = (vc[:, (H + h) * P:(H + h + 1) * P], vs[:, (H + h) * P:(H + h + 1) * P])
-            lo = tuple(a[:, h * P:(h + 1) * P] for a in vlo[b % 2])
-            hi = tuple(a[:, h * P:(h + 1) * P] for a in vhi[b % 2])
-            plan = (((0, past), (1, lo)), ((2, past), (1, hi)), ((0, past), (1, new)), ((2, past), (3, new)))
-            for t in range(t0, t0 + nt):
-                ec = st[("ec", b, h, t // 2)]
-                es = st[("es", b, h, t // 2)]
-                for i, (c, (rc, rs)) in enumerate(plan[t]):
+            full = (st[("vcodes", b)], vscales[b % 2])
+            sub = vsub[b % 2]
+            for j, t in enumerate(tiles):
+                passes = [(h, ("past", t), full, h * P)]
+                if t == 0:
+                    passes.append((h, ("new", 2), sub["hi32"], h * P))
+                if t == 1:
+                    passes.append((h + 1 - h % 2, ("new", 1), sub["half"], h * P))
+                if t == 2:
+                    passes.append((h, ("new", 2), sub["lo96"], h * P))
+                if t == 3:
+                    passes.append((h, ("new", 3), full, (H + h) * P))
+                for i, (eh, block, (vc, vs), c0) in enumerate(passes):
+                    g = st[("blocks", b, eh)].index(block)
                     nc.tensor.matmul_mx(
-                        out=ops[:, (t - t0) * P:(t - t0 + 1) * P],
-                        lhsT=ec[:, c * P:(c + 1) * P].bitcast(FP8X4),
-                        lhsT_scale=es[:, c * P:(c + 1) * P],
-                        rhs=rc.bitcast(FP8X4),
-                        rhs_scale=rs,
+                        out=ops[:, j * P:(j + 1) * P],
+                        lhsT=st[("ec", b, eh)][:, g * P:(g + 1) * P].bitcast(FP8X4),
+                        lhsT_scale=st[("es", b, eh)][:, g * P:(g + 1) * P],
+                        rhs=vc[:, c0:c0 + P].bitcast(FP8X4),
+                        rhs_scale=vs[:, c0:c0 + P],
                         start=(i == 0), stop=(i == 1),
                     )
             return ops
 
-        def finish_tiles(ops, b, h, t0, nt, on_scalar):
+        def finish_tiles(ops, b, h, tiles, on_scalar):
+            nt = len(tiles)
+            ts = slice(tiles[0], tiles[-1] + 1, tiles[1] - tiles[0])
             rc = small.tile([P, NT], F32, name="rc")
-            nc.gpsimd.tensor_tensor(
-                out=rc[:, 0:nt], in0=st[("rs", b, h)][:, t0:t0 + nt], in1=minus_one[:, 0:nt], op=ALU.pow
-            )
+            nc.gpsimd.tensor_tensor(out=rc[:, 0:nt], in0=st[("rs", b, h)][:, ts], in1=minus_one[:, 0:nt], op=ALU.pow)
             o_sb = work.tile([P, NT * P], F32, name="o_sb")
             if on_scalar:
                 for i in range(nt):
@@ -355,16 +376,30 @@ def tile_flashattentionmodule_pa_t_kernel(tc, x, q, k_new, past_k, past_v, Wv, b
                     op=ALU.mult,
                 )
             nc.sync.dma_start(
-                out=out[b, t0 * P:(t0 + nt) * P, h * P:(h + 1) * P].rearrange("(t p) d -> p t d", p=P),
+                out=out[b, :, h * P:(h + 1) * P].rearrange("(t p) d -> p t d", p=P)[:, ts],
                 in_=o_sb[:, 0:nt * P].rearrange("p (t d) -> p t d", t=nt),
             )
 
         heads = [(b, h) for b in range(B) for h in range(H)]
-        steps = [(b, h, t) for (b, h) in heads for t in ((2, 3, 0, 1) if (b, h) == heads[-1] else range(NT))]
+        order = {hd: (0, 2, 1, 3) for hd in heads}
+        order[heads[-1]] = (1, 3, 2, 0)
+        steps = [(b, h, t) for (b, h) in heads for t in order[(b, h)]]
         n_steps = len(steps)
-        quant_at = {(b, h, i): steps.index((b, h, 2 * i + 1)) + QLAG for (b, h) in heads for i in range(2)}
+        quants = {}
+        ready = {}
+        for (b, h) in heads:
+            last = (b, h) == heads[-1]
+            first_row = steps.index((b, h, 3 if last else 1)) + QLAG
+            second_row = n_steps + 1 if last else steps.index((b, h, 3)) + QLAG
+            quants.setdefault(first_row, []).append((b, h, 0, 4))
+            if last:
+                quants.setdefault(second_row, []).extend([(b, h, 4, 2), (b, h, 6, 1)])
+            else:
+                if h % 2 == 1:
+                    quants.setdefault(first_row, []).append((b, h, 4, 1))
+                quants.setdefault(second_row, []).append((b, h, 4 + h % 2, 2))
+            ready[(b, h)] = (first_row, second_row)
         late_e = range(n_steps - 4, n_steps - 1)
-        quant_at[(B - 1, H - 1, 0)] = n_steps + 1
 
         def warm(count):
             junk = psum.tile([P, 512], F32, name="junk", tag="sA", bufs=2)
@@ -379,10 +414,14 @@ def tile_flashattentionmodule_pa_t_kernel(tc, x, q, k_new, past_k, past_v, Wv, b
         value_jobs = [("x", 0, 0), ("x", 0, 1), ("bias", 0, 0)] + [("vn", 0, h) for h in range(H)]
         for b in range(1, B):
             value_jobs += [("x", b, 0), ("x", b, 1)] + [("vn", b, h) for h in range(H)]
-        pv_jobs = [("pv", b, (h, 0, NT)) for (b, h) in heads[:-1]]
-        pv_jobs += [("pv", B - 1, (H - 1, 2, 2)), ("pv", B - 1, (H - 1, 0, 2))]
+        pv_jobs = []
+        for (b, h) in heads[:-1]:
+            at = ready[(b, h)][1] if h % 2 == 1 else max(ready[(b, h)][1], ready[(b, h + 1)][0])
+            pv_jobs.append(("pv", b, (h, (0, 1, 2, 3), at + 1)))
+        pv_jobs.append(("pv", B - 1, (H - 1, (1, 3), ready[heads[-1]][0] + 1)))
+        pv_jobs.append(("pv", B - 1, (H - 1, (0, 2), ready[heads[-1]][1])))
 
-        def job_transposes(job, n, tag, sout, after):
+        def job_transposes(job, n, tag, sout, early, after):
             kind, b, j = job
             if kind == "x":
                 if j == 0 and b > 0:
@@ -392,9 +431,9 @@ def tile_flashattentionmodule_pa_t_kernel(tc, x, q, k_new, past_k, past_v, Wv, b
                 tp = words_pe(st[("x", b)], j, tag, 1)
                 sout.append(lambda: words_out(tp, st[("xgrp", b)], j, nc.scalar.copy))
                 if j == 1:
-                    after.setdefault(n + 2, []).append(lambda: x_quant(b))
-                    after.setdefault(n + 3, []).append(lambda: v_quant(b, 0))
-                    st[("ready", "vn", b)] = n + 3
+                    early.setdefault(n + 4, []).append(lambda: x_quant(b))
+                    after.setdefault(n + 4, []).append(lambda: v_quant(b, 0))
+                    st[("ready", "vn", b)] = n + 4
 
         def job_matmuls(job, n, tag, outs, sout, after):
             kind, b, j = job
@@ -409,18 +448,15 @@ def tile_flashattentionmodule_pa_t_kernel(tc, x, q, k_new, past_k, past_v, Wv, b
                     after.setdefault(n + 2, []).append(lambda: v_move(b))
                     st[("ready", "pv", b)] = n + 5
             if kind == "pv":
-                ops = pv_tiles(b, j[0], j[1], j[2], tag)
+                ops = pv_tiles(b, j[0], j[1], tag)
                 on_scalar = j[0] in FINISH_ON_SCALAR and b < B - 1
-                (sout if on_scalar else outs).append(lambda: finish_tiles(ops, b, j[0], j[1], j[2], on_scalar))
+                (sout if on_scalar else outs).append(lambda: finish_tiles(ops, b, j[0], j[1], on_scalar))
 
         def next_job(n, t):
             pv_ready = False
             if pv_jobs:
                 kind, b, j = pv_jobs[0]
-                pv_ready = (
-                    st.get(("ready", "pv", b), n_steps) <= n
-                    and quant_at[(b, j[0], (j[1] + j[2] - 1) // 2)] + (n < n_steps) <= n
-                )
+                pv_ready = st.get(("ready", "pv", b), n_steps) <= n and j[2] <= n
             value_ready = bool(value_jobs) and pv_jobs[0][1] >= value_jobs[0][1] - 1
             if value_ready and value_jobs[0][0] == "vn":
                 value_ready = st[("ready", "vn", value_jobs[0][1])] <= n
@@ -463,12 +499,14 @@ def tile_flashattentionmodule_pa_t_kernel(tc, x, q, k_new, past_k, past_v, Wv, b
             pv_group(0, h)
         for i in range(2):
             nc.gpsimd.memset(vscales[i][:].bitcast(U32), 0)
-            for c, s in (vlo[i], vhi[i]):
+        for i in range(2):
+            for c, s in vsub[i].values():
                 nc.gpsimd.memset(c[:], 0)
                 nc.gpsimd.memset(s[:].bitcast(U32), 0)
 
         outs = []
         sout = []
+        early = {}
         after = {0: [lambda: nc.vector.quantize_mx(out=wcodes[:].bitcast(FP8X4), scales=wscales[:], in_=wgrp[:])]}
         q_wait = []
         for n in range(n_steps + 40):
@@ -477,8 +515,10 @@ def tile_flashattentionmodule_pa_t_kernel(tc, x, q, k_new, past_k, past_v, Wv, b
             b, h, t = steps[min(n, n_steps - 1)]
             hi = heads.index((b, h))
             t = n % NT
-            for pair in [p for p in quant_at if quant_at[p] == n]:
-                e_quant(*pair)
+            for fn in early.pop(n, []):
+                fn()
+            for group in quants.get(n, ()):
+                e_quant(*group)
             for hd in q_wait:
                 q_out(*hd, nc.scalar.copy)
             q_wait = []
@@ -496,7 +536,7 @@ def tile_flashattentionmodule_pa_t_kernel(tc, x, q, k_new, past_k, past_v, Wv, b
             if n == n_steps - 1:
                 tag = None
             job = next_job(n, t) if tag else ("none", 0, 0)
-            job_transposes(job, n, tag, sout, after)
+            job_transposes(job, n, tag, sout, early, after)
             if n + 4 < n_steps:
                 scores_past(*steps[n + 4])
             job_matmuls(job, n, tag, outs, sout, after)

@@ -25,7 +25,8 @@ BLOCKS = 7
 QLAG = 3
 FINISH_ON_SCALAR = (0,)
 JOB_BANK = (None, "ops", "tr", "ops")
-LOAD_STEPS = ((3, 6, 8), (12, 4, 8))
+FIRST_LOADS = {3: (0, 1), 4: (2, 3), 6: ("x",), 8: ("pv",)}
+LATER_LOADS = {1: ("x",), 3: ("pv",), 6: (0,), 8: (1,), 10: (2,), 12: (3,)}
 
 
 def tile_flashattentionmodule_pa_t_kernel(tc, x, q, k_new, past_k, past_v, Wv, bv, out):
@@ -104,11 +105,11 @@ def tile_flashattentionmodule_pa_t_kernel(tc, x, q, k_new, past_k, past_v, Wv, b
         wcodes = consts.tile([P, D], U32, name="wcodes", align_bytes=64)
         wscales = consts.tile([P, D], U8, name="wscales", align_bytes=64)
         vscales = []
-        for i in range(2):
+        for i in range(3):
             vs_t = consts.tile([P, 2 * H * HD], U8, name="vscales%d" % i, align_bytes=64)
             vscales.append(vs_t)
         vsub = []
-        for i in range(2):
+        for i in range(3):
             sub = {}
             for key in ("lo96", "hi32", "half"):
                 c = consts.tile([P, H * HD], U32, name="%s_c%d" % (key, i), align_bytes=64)
@@ -141,7 +142,7 @@ def tile_flashattentionmodule_pa_t_kernel(tc, x, q, k_new, past_k, past_v, Wv, b
             st[("xcodes", b)] = batchp.tile([P, D], U32, name="xcodes", align_bytes=64)
             st[("xscales", b)] = batchp.tile([P, D], U8, name="xscales", align_bytes=64)
             st[("vgrp", b)] = batchp.tile([P, 2 * H * HD * 4], BF16, name="vgrp", align_bytes=64)
-            st[("vcodes", b)] = batchp.tile([P, 2 * H * HD], U32, name="vcodes", align_bytes=64)
+            st[("vcodes", b)] = batchp.tile([P, 2 * H * HD], U32, name="vcodes", align_bytes=64, bufs=3)
 
         def x_quant(b):
             nc.vector.quantize_mx(
@@ -157,13 +158,13 @@ def tile_flashattentionmodule_pa_t_kernel(tc, x, q, k_new, past_k, past_v, Wv, b
         def v_quant(b, g):
             nc.vector.quantize_mx(
                 out=st[("vcodes", b)][:, g * 512:(g + 1) * 512].bitcast(FP8X4),
-                scales=vscales[b % 2][:, g * 512:(g + 1) * 512],
+                scales=vscales[b % 3][:, g * 512:(g + 1) * 512],
                 in_=st[("vgrp", b)][:, g * 2048:(g + 1) * 2048],
             )
 
         def v_move(b):
-            sub = vsub[b % 2]
-            for i, src in enumerate((st[("vcodes", b)], vscales[b % 2])):
+            sub = vsub[b % 3]
+            for i, src in enumerate((st[("vcodes", b)], vscales[b % 3])):
                 new = src[:, 512:1024].bitcast(I32)
                 nc.sync.dma_start(out=sub["lo96"][i][0:96, :].bitcast(I32), in_=new[0:96, :])
                 nc.sync.dma_start(out=sub["hi32"][i][96:P, :].bitcast(I32), in_=new[0:32, :])
@@ -332,8 +333,8 @@ def tile_flashattentionmodule_pa_t_kernel(tc, x, q, k_new, past_k, past_v, Wv, b
 
         def pv_tiles(b, h, tiles, tag):
             ops = psum.tile([P, 512], F32, name="ops", tag=tag)
-            full = (st[("vcodes", b)], vscales[b % 2])
-            sub = vsub[b % 2]
+            full = (st[("vcodes", b)], vscales[b % 3])
+            sub = vsub[b % 3]
             for j, t in enumerate(tiles):
                 passes = [(h, ("past", t), full, h * P)]
                 if t == 0:
@@ -446,7 +447,7 @@ def tile_flashattentionmodule_pa_t_kernel(tc, x, q, k_new, past_k, past_v, Wv, b
                 if j == H - 1:
                     after.setdefault(n + 2, []).append(lambda: v_quant(b, 1))
                     after.setdefault(n + 2, []).append(lambda: v_move(b))
-                    st[("ready", "pv", b)] = n + 5
+                    st[("ready", "pv", b)] = n + 7
             if kind == "pv":
                 ops = pv_tiles(b, j[0], j[1], tag)
                 on_scalar = j[0] in FINISH_ON_SCALAR and b < B - 1
@@ -457,7 +458,7 @@ def tile_flashattentionmodule_pa_t_kernel(tc, x, q, k_new, past_k, past_v, Wv, b
             if pv_jobs:
                 kind, b, j = pv_jobs[0]
                 pv_ready = st.get(("ready", "pv", b), n_steps) <= n and j[2] <= n
-            value_ready = bool(value_jobs) and pv_jobs[0][1] >= value_jobs[0][1] - 1
+            value_ready = bool(value_jobs) and min(pv_jobs[0][1] + 2, n // 16 + 1) >= value_jobs[0][1]
             if value_ready and value_jobs[0][0] == "vn":
                 value_ready = st[("ready", "vn", value_jobs[0][1])] <= n
             if pv_ready and (t == 3 or not value_ready):
@@ -497,9 +498,9 @@ def tile_flashattentionmodule_pa_t_kernel(tc, x, q, k_new, past_k, past_v, Wv, b
         scores_past(*steps[3])
         for h in range(H):
             pv_group(0, h)
-        for i in range(2):
+        for i in range(3):
             nc.gpsimd.memset(vscales[i][:].bitcast(U32), 0)
-        for i in range(2):
+        for i in range(3):
             for c, s in vsub[i].values():
                 nc.gpsimd.memset(c[:], 0)
                 nc.gpsimd.memset(s[:].bitcast(U32), 0)
@@ -558,15 +559,15 @@ def tile_flashattentionmodule_pa_t_kernel(tc, x, q, k_new, past_k, past_v, Wv, b
                 fn()
             for fn in after.pop(n, []):
                 fn()
-            for c, s in ((1, n), (b + 2, 4 * h + t)):
-                if c >= B or n >= n_steps:
-                    continue
-                if s == LOAD_STEPS[c > 1][0]:
-                    load_tiles(c, ("pk", "kn", "q"))
-                    load_qk(c, 0, H)
-                if s == LOAD_STEPS[c > 1][1]:
-                    load_tiles(c, ("x",))
-                    load_x(c)
-                if s == LOAD_STEPS[c > 1][2]:
-                    load_tiles(c, ("pv",))
-                    load_pv(c)
+            for c, s, plan in ((1, n, FIRST_LOADS), (b + 2, 4 * h + t, LATER_LOADS)):
+                for what in plan.get(s, ()) if c < B and n < n_steps else ():
+                    if what == "x":
+                        load_tiles(c, ("x",))
+                        load_x(c)
+                    elif what == "pv":
+                        load_tiles(c, ("pv",))
+                        load_pv(c)
+                    else:
+                        if what == 0:
+                            load_tiles(c, ("pk", "kn", "q"))
+                        load_qk(c, what, what + 1)

@@ -24,7 +24,7 @@ E_COLS = 3 * S
 BLOCKS = 7
 QLAG = 3
 FINISH_ON_SCALAR = (0,)
-JOB_BANK = (None, "ops", "tr", "ops")
+JOB_BANK = ("ops", None, "ops", "tr")
 FIRST_LOADS = {3: (0, 1), 4: (2, 3), 6: ("x",), 8: ("pv",)}
 LATER_LOADS = {1: ("x",), 3: ("pv",), 6: (0,), 8: (1,), 10: (2,), 12: (3,)}
 
@@ -96,14 +96,6 @@ def tile_flashattentionmodule_pa_t_kernel(tc, x, q, k_new, past_k, past_v, Wv, b
         e02 = consts.tile([P, E_COLS], BF16, name="e02")
         e11 = consts.tile([P, E_COLS], BF16, name="e11")
         e3 = consts.tile([P, T], BF16, name="e3")
-        mask_bf = consts.tile([P, P], BF16, name="mask_bf")
-        nc.vector.tensor_copy(out=mask_bf[:], in_=mask_f[:])
-        minus_one = consts.tile([P, NT], F32, name="minus_one")
-        nc.vector.memset(minus_one[:], -1.0)
-        bias_f = consts.tile([P, D], F32, name="bias_f")
-        wgrp = consts.tile([P, 4 * D], BF16, name="wgrp", align_bytes=64)
-        wcodes = consts.tile([P, D], U32, name="wcodes", align_bytes=64)
-        wscales = consts.tile([P, D], U8, name="wscales", align_bytes=64)
         vscales = []
         for i in range(3):
             vs_t = consts.tile([P, 2 * H * HD], U8, name="vscales%d" % i, align_bytes=64)
@@ -116,7 +108,19 @@ def tile_flashattentionmodule_pa_t_kernel(tc, x, q, k_new, past_k, past_v, Wv, b
                 s = consts.tile([P, H * HD], U8, name="%s_s%d" % (key, i), align_bytes=64)
                 sub[key] = (c, s)
             vsub.append(sub)
-
+        for i in range(3):
+            nc.vector.memset(vscales[i][:].bitcast(U32), 0)
+            for c, sc in vsub[i].values():
+                nc.vector.memset(c[:], 0)
+                nc.vector.memset(sc[:].bitcast(U32), 0)
+        mask_bf = consts.tile([P, P], BF16, name="mask_bf")
+        nc.vector.tensor_copy(out=mask_bf[:], in_=mask_f[:])
+        minus_one = consts.tile([P, NT], F32, name="minus_one")
+        nc.vector.memset(minus_one[:], -1.0)
+        bias_f = consts.tile([P, D], F32, name="bias_f")
+        wgrp = consts.tile([P, 4 * D], BF16, name="wgrp", align_bytes=64)
+        wcodes = consts.tile([P, D], U32, name="wcodes", align_bytes=64)
+        wscales = consts.tile([P, D], U8, name="wscales", align_bytes=64)
         def words_pe(src, half, tag, bufs):
             s32 = src[:].bitcast(F32)
             tp = psum.tile([P, 512], F32, name="tp", tag=tag, bufs=bufs)
@@ -226,8 +230,10 @@ def tile_flashattentionmodule_pa_t_kernel(tc, x, q, k_new, past_k, past_v, Wv, b
             st[("qT", b, h)] = qT
             st[("rs", b, h)] = headp.tile([P, NT], F32, name="rs", bufs=8)
 
-        def scores_past(b, h, t):
+        def scores_past(b, h, t, extra=0):
             sA = psum.tile([P, 512], F32, name="sA", bufs=2)
+            for i in range(extra):
+                nc.tensor.matmul(sA[:, 0:P], lhsT=ones_bf[:], rhs=ones_bf[:], start=True, stop=True)
             nc.tensor.matmul(
                 sA[:], lhsT=st[("qT", b, h)][:, t * P:(t + 1) * P], rhs=st[("kT", b, h)][:, 0:S], start=True, stop=True
             )
@@ -461,7 +467,7 @@ def tile_flashattentionmodule_pa_t_kernel(tc, x, q, k_new, past_k, past_v, Wv, b
             value_ready = bool(value_jobs) and min(pv_jobs[0][1] + 2, n // 16 + 1) >= value_jobs[0][1]
             if value_ready and value_jobs[0][0] == "vn":
                 value_ready = st[("ready", "vn", value_jobs[0][1])] <= n
-            if pv_ready and (t == 3 or not value_ready):
+            if pv_ready and (t == 2 or not value_ready):
                 return pv_jobs.pop(0)
             if value_ready:
                 return value_jobs.pop(0)
@@ -498,12 +504,6 @@ def tile_flashattentionmodule_pa_t_kernel(tc, x, q, k_new, past_k, past_v, Wv, b
         scores_past(*steps[3])
         for h in range(H):
             pv_group(0, h)
-        for i in range(3):
-            nc.gpsimd.memset(vscales[i][:].bitcast(U32), 0)
-        for i in range(3):
-            for c, s in vsub[i].values():
-                nc.gpsimd.memset(c[:], 0)
-                nc.gpsimd.memset(s[:].bitcast(U32), 0)
 
         outs = []
         sout = []
@@ -528,9 +528,9 @@ def tile_flashattentionmodule_pa_t_kernel(tc, x, q, k_new, past_k, past_v, Wv, b
             if 0 <= n - 1 < n_steps:
                 e_pe(*steps[n - 1])
             if n < n_steps and hi + 2 < len(heads):
-                if t == 0:
-                    k_pe(*heads[hi + 2])
                 if t == 1:
+                    k_pe(*heads[hi + 2])
+                if t == 2:
                     q_pe(*heads[hi + 2], "tr", 1)
                     q_wait.append(heads[hi + 2])
             tag = JOB_BANK[t] if n < n_steps else ("tr", "ops")[n % 2]
@@ -539,7 +539,7 @@ def tile_flashattentionmodule_pa_t_kernel(tc, x, q, k_new, past_k, past_v, Wv, b
             job = next_job(n, t) if tag else ("none", 0, 0)
             job_transposes(job, n, tag, sout, early, after)
             if n + 4 < n_steps:
-                scores_past(*steps[n + 4])
+                scores_past(*steps[n + 4], extra=4 if t in (1, 3) and job[0] in ("none", "x") else 0)
             job_matmuls(job, n, tag, outs, sout, after)
             if n + 3 < n_steps:
                 scores_new(*steps[n + 3])
@@ -547,7 +547,7 @@ def tile_flashattentionmodule_pa_t_kernel(tc, x, q, k_new, past_k, past_v, Wv, b
                 expo(*steps[n])
             if 0 <= n - 1 < n_steps:
                 e_out(*steps[n - 1], nc.vector.tensor_copy if n - 1 in late_e else nc.scalar.copy)
-            if n < n_steps and hi + 2 < len(heads) and t == 0:
+            if n < n_steps and hi + 2 < len(heads) and t == 1:
                 k_out(*heads[hi + 2])
             for fn in snow:
                 fn()

@@ -400,7 +400,8 @@ def tile_flashattentionmodule_pa_t_kernel(tc, x, q, k_new, past_k, past_v, Wv, b
             second_row = n_steps + 1 if last else steps.index((b, h, 3)) + QLAG
             quants.setdefault(first_row, []).append((b, h, 0, 4))
             if last:
-                quants.setdefault(second_row, []).extend([(b, h, 4, 2), (b, h, 6, 1)])
+                quants.setdefault(n_steps, []).append((b, h, 4, 1))
+                quants.setdefault(second_row, []).append((b, h, 5, 2))
             else:
                 if h % 2 == 1:
                     quants.setdefault(first_row, []).append((b, h, 4, 1))
@@ -545,18 +546,18 @@ def tile_flashattentionmodule_pa_t_kernel(tc, x, q, k_new, past_k, past_v, Wv, b
                 scores_new(*steps[n + 3])
             if n < n_steps:
                 expo(*steps[n])
+            for fn in snow:
+                fn()
             if 0 <= n - 1 < n_steps:
                 e_out(*steps[n - 1], nc.vector.tensor_copy if n - 1 in late_e else nc.scalar.copy)
             if n < n_steps and hi + 2 < len(heads) and t == 1:
                 k_out(*heads[hi + 2])
-            for fn in snow:
-                fn()
             if n + 3 < n_steps:
                 rowmax_past(*steps[n + 3])
-            if n + 2 < n_steps:
-                rowmax_new(*steps[n + 2])
             for fn in now:
                 fn()
+            if n + 2 < n_steps:
+                rowmax_new(*steps[n + 2])
             for fn in after.pop(n, []):
                 fn()
             for c, s, plan in ((1, n, FIRST_LOADS), (b + 2, 4 * h + t, LATER_LOADS)):

import math
from contextlib import ExitStack

import concourse.mybir as mybir
from concourse.masks import make_identity

BF16 = mybir.dt.bfloat16
F32 = mybir.dt.float32
U32 = mybir.dt.uint32
I32 = mybir.dt.int32
U8 = mybir.dt.uint8
FP8X4 = mybir.dt.float8_e4m3fn_x4
ALU = mybir.AluOpType
ACT = mybir.ActivationFunctionType

P = 128
B, S, D, H, HD = 8, 512, 512, 4, 128
T = 2 * S
NT = S // P
SCALE = 1.0 / math.sqrt(HD)
MASK = -1.0e30
FLOPS = 2 * B * S * D * D + 2 * 2 * B * H * S * T * HD
E_COLS = 3 * S
BLOCKS = 7
QLAG = 3
FINISH_ON_SCALAR = (0,)
JOB_BANK = ("ops", None, "ops", "tr")
FIRST_LOADS = {3: (0, 1), 4: (2, 3), 6: ("x",), 8: ("pv",)}
LATER_LOADS = {1: ("x",), 3: ("pv",), 6: (0,), 8: (1,), 10: (2,), 12: (3,)}


def tile_flashattentionmodule_pa_t_kernel(tc, x, q, k_new, past_k, past_v, Wv, bv, out):
    nc = tc.nc
    with ExitStack() as ctx:
        consts = ctx.enter_context(tc.tile_pool(name="consts", bufs=1))
        loads = ctx.enter_context(tc.tile_pool(name="loads", bufs=2))
        batchp = ctx.enter_context(tc.tile_pool(name="batchp", bufs=2))
        headp = ctx.enter_context(tc.tile_pool(name="headp", bufs=2))
        work = ctx.enter_context(tc.tile_pool(name="work", bufs=3))
        small = ctx.enter_context(tc.tile_pool(name="small", bufs=8))
        psum = ctx.enter_context(tc.psum_pool(name="psum", bufs=1))
        ctx.enter_context(tc.manual_schedule())

        st = {}

        def load_qk(b, h0, h1):
            for key, src in (("q", q), ("pk", past_k), ("kn", k_new)):
                nc.sync.dma_start(
                    out=st[(key, b)][:, h0 * S:h1 * S].rearrange("p (h a d) -> p h a d", h=h1 - h0, a=NT),
                    in_=src[b, h0:h1].rearrange("h (a p) d -> p h a d", p=P),
                )

        def load_x(b):
            nc.sync.dma_start(
                out=st[("x", b)][:].rearrange("p (j f) -> p j f", j=4),
                in_=x[b].rearrange("(m j) f -> m j f", j=4),
            )

        def load_pv(b):
            nc.sync.dma_start(
                out=st[("pv", b)][:].rearrange("p (h u e d) -> p h u e d", h=H, u=2, e=2),
                in_=past_v[b].rearrange("h (u m e) d -> m h u e d", u=2, e=2),
            )

        def load_tiles(b, keys):
            for key in keys:
                st[(key, b)] = loads.tile([P, H * S], BF16, name=key + "_sb")

        load_tiles(0, ("x", "pv", "pk", "kn", "q"))
        load_qk(0, 0, 1)
        load_qk(0, 1, 2)
        w_sb = consts.tile([P, 4 * D], BF16, name="w_sb")
        nc.sync.dma_start(
            out=w_sb[:].rearrange("p (o f) -> p o f", o=4),
            in_=Wv.rearrange("(o p) f -> p o f", p=P),
        )
        load_x(0)
        load_qk(0, 2, 3)
        load_pv(0)
        load_qk(0, 3, H)
        ident_bf = consts.tile([P, P], BF16, name="ident_bf")
        make_identity(nc, ident_bf[:])
        mask_f = consts.tile([P, P], F32, name="mask_f")
        nc.gpsimd.memset(mask_f[:], 0.0)
        nc.gpsimd.affine_select(
            out=mask_f[:], in_=mask_f[:], compare_op=ALU.is_ge, fill=MASK,
            base=0, pattern=[[-1, P]], channel_multiplier=1,
        )
        ident_f = consts.tile([P, P], F32, name="ident_f")
        make_identity(nc, ident_f[:])
        ones_bf = consts.tile([P, P], BF16, name="ones_bf")
        nc.vector.memset(ones_bf[:], 1.0)
        bias_bf = consts.tile([P, D], BF16, name="bias_bf")
        nc.vector.memset(bias_bf[:], 0.0)
        nc.sync.dma_start(out=bias_bf[0:1, :], in_=bv.rearrange("(o n) -> o n", o=1))
        e02 = consts.tile([P, E_COLS], BF16, name="e02")
        e11 = consts.tile([P, E_COLS], BF16, name="e11")
        e3 = consts.tile([P, T], BF16, name="e3")
        vscales = []
        for i in range(3):
            vs_t = consts.tile([P, 2 * H * HD], U8, name="vscales%d" % i, align_bytes=64)
            vscales.append(vs_t)
        vsub = []
        for i in range(3):
            sub = {}
            for key in ("lo96", "hi32", "half"):
                c = consts.tile([P, H * HD], U32, name="%s_c%d" % (key, i), align_bytes=64)
                s = consts.tile([P, H * HD], U8, name="%s_s%d" % (key, i), align_bytes=64)
                sub[key] = (c, s)
            vsub.append(sub)
        for i in range(3):
            nc.vector.memset(vscales[i][:].bitcast(U32), 0)
            for c, sc in vsub[i].values():
                nc.vector.memset(c[:], 0)
                nc.vector.memset(sc[:].bitcast(U32), 0)
        mask_bf = consts.tile([P, P], BF16, name="mask_bf")
        nc.vector.tensor_copy(out=mask_bf[:], in_=mask_f[:])
        minus_one = consts.tile([P, NT], F32, name="minus_one")
        nc.vector.memset(minus_one[:], -1.0)
        bias_f = consts.tile([P, D], F32, name="bias_f")
        wgrp = consts.tile([P, 4 * D], BF16, name="wgrp", align_bytes=64)
        wcodes = consts.tile([P, D], U32, name="wcodes", align_bytes=64)
        wscales = consts.tile([P, D], U8, name="wscales", align_bytes=64)
        def words_pe(src, half, tag, bufs):
            s32 = src[:].bitcast(F32)
            tp = psum.tile([P, 512], F32, name="tp", tag=tag, bufs=bufs)
            for oo in range(2):
                for u in range(2):
                    o = 2 * half + oo
                    nc.tensor.transpose(
                        tp[:, (oo * 2 + u) * P:(oo * 2 + u + 1) * P],
                        s32[:, o * 256 + u * P:o * 256 + (u + 1) * P],
                        ident_f[:],
                    )
            return tp

        def words_out(tp, grp, half, copy_fn):
            g32 = grp[:].bitcast(F32).rearrange("p (o m u) -> p o m u", o=4, u=2)
            copy_fn(
                out=g32[:, 2 * half:2 * half + 2],
                in_=tp[:].rearrange("p (o u m) -> p o m u", o=2, u=2),
            )

        def batch_tiles(b):
            st[("xgrp", b)] = batchp.tile([P, 4 * D], BF16, name="xgrp", align_bytes=64)
            st[("xcodes", b)] = batchp.tile([P, D], U32, name="xcodes", align_bytes=64)
            st[("xscales", b)] = batchp.tile([P, D], U8, name="xscales", align_bytes=64)
            st[("vgrp", b)] = batchp.tile([P, 2 * H * HD * 4], BF16, name="vgrp", align_bytes=64)
            st[("vcodes", b)] = batchp.tile([P, 2 * H * HD], U32, name="vcodes", align_bytes=64, bufs=3)

        def x_quant(b):
            nc.vector.quantize_mx(
                out=st[("xcodes", b)][:].bitcast(FP8X4), scales=st[("xscales", b)][:], in_=st[("xgrp", b)][:]
            )

        def pv_group(b, h):
            vg = st[("vgrp", b)]
            dst = vg[:, h * 512:(h + 1) * 512].rearrange("p (d t) -> p d t", t=4)
            src = st[("pv", b)][:, h * 512:(h + 1) * 512].rearrange("p (t d) -> p d t", t=4)
            nc.gpsimd.tensor_scalar(out=dst, in0=src, scalar1=1.0, scalar2=0.0, op0=ALU.mult, op1=ALU.add)

        def v_quant(b, g):
            nc.vector.quantize_mx(
                out=st[("vcodes", b)][:, g * 512:(g + 1) * 512].bitcast(FP8X4),
                scales=vscales[b % 3][:, g * 512:(g + 1) * 512],
                in_=st[("vgrp", b)][:, g * 2048:(g + 1) * 2048],
            )

        def v_move(b):
            sub = vsub[b % 3]
            for i, src in enumerate((st[("vcodes", b)], vscales[b % 3])):
                new = src[:, 512:1024].bitcast(I32)
                nc.sync.dma_start(out=sub["lo96"][i][0:96, :].bitcast(I32), in_=new[0:96, :])
                nc.sync.dma_start(out=sub["hi32"][i][96:P, :].bitcast(I32), in_=new[0:32, :])
                by_head = new.rearrange("p (g a d) -> p g a d", g=2, a=2)
                half = sub["half"][i][:].bitcast(I32).rearrange("p (g a d) -> p g a d", g=2, a=2)
                for a in range(2):
                    nc.sync.dma_start(out=half[64 * a:64 * (a + 1), :, a], in_=by_head[0:64, :, a])

        def vnew_pe(b, h, tag):
            vn = psum.tile([P, 512], F32, name="vn", tag=tag)
            xc = st[("xcodes", b)]
            xs = st[("xscales", b)]
            for tau in range(4):
                nc.tensor.matmul_mx(
                    out=vn[:, tau * P:(tau + 1) * P],
                    lhsT=xc[:, tau * P:(tau + 1) * P].bitcast(FP8X4),
                    lhsT_scale=xs[:, tau * P:(tau + 1) * P],
                    rhs=wcodes[:, h * P:(h + 1) * P].bitcast(FP8X4),
                    rhs_scale=wscales[:, h * P:(h + 1) * P],
                    start=True, stop=True,
                )
            return vn

        def vnew_out(vn, b, h):
            vg = st[("vgrp", b)]
            nc.vector.tensor_tensor(
                out=vg[:, 2048 + h * 512:2048 + (h + 1) * 512].rearrange("p (d t) -> p d t", t=4),
                in0=vn[:].rearrange("p (t d) -> p d t", t=4),
                in1=bias_f[:, h * P:(h + 1) * P].unsqueeze(2).to_broadcast([P, P, 4]),
                op=ALU.add,
            )

        def half_pe(key, b, h, ktp, c0):
            for a in range(NT):
                nc.tensor.transpose(
                    ktp[:, c0 + a * P:c0 + (a + 1) * P], st[(key, b)][:, (h * NT + a) * P:(h * NT + a + 1) * P],
                    ident_bf[:],
                )

        def k_pe(b, h):
            ktp = psum.tile([P, T], BF16, name="ktp", tag="tr")
            half_pe("pk", b, h, ktp, 0)
            half_pe("kn", b, h, ktp, S)
            st[("ktp", b, h)] = ktp

        def k_out(b, h):
            kT = headp.tile([P, T], BF16, name="kT", bufs=3)
            nc.scalar.copy(out=kT[:], in_=st[("ktp", b, h)][:])
            st[("kT", b, h)] = kT

        def q_pe(b, h, tag, bufs):
            qtp = psum.tile([P, S], BF16, name="qtp", tag=tag, bufs=bufs)
            half_pe("q", b, h, qtp, 0)
            st[("qtp", b, h)] = qtp

        def q_out(b, h, copy_fn):
            qT = headp.tile([P, S], BF16, name="qT", bufs=3)
            copy_fn(out=qT[:], in_=st[("qtp", b, h)][:])
            st[("qT", b, h)] = qT
            st[("rs", b, h)] = headp.tile([P, NT], F32, name="rs", bufs=8)

        def scores_past(b, h, t, extra=0):
            sA = psum.tile([P, 512], F32, name="sA", bufs=2)
            for i in range(extra):
                nc.tensor.matmul(sA[:, 0:P], lhsT=ones_bf[:], rhs=ones_bf[:], start=True, stop=True)
            nc.tensor.matmul(
                sA[:], lhsT=st[("qT", b, h)][:, t * P:(t + 1) * P], rhs=st[("kT", b, h)][:, 0:S], start=True, stop=True
            )
            st[("sA", b, h, t)] = sA

        def scores_new(b, h, t):
            sB = psum.tile([P, 512], F32, name="sB", bufs=2)
            kT = st[("kT", b, h)]
            lq = st[("qT", b, h)][:, t * P:(t + 1) * P]
            if t > 0:
                nc.tensor.matmul(sB[:, 0:t * P], lhsT=lq, rhs=kT[:, S:S + t * P], start=True, stop=True)
            nc.tensor.matmul(
                sB[:, t * P:(t + 1) * P], lhsT=lq, rhs=kT[:, S + t * P:S + (t + 1) * P], start=True, stop=False
            )
            nc.tensor.matmul(sB[:, t * P:(t + 1) * P], lhsT=ident_bf[:], rhs=mask_bf[:], start=False, stop=True)
            st[("sB", b, h, t)] = sB

        def new_first(h, t):
            return t == 0 or (t == 1 and h % 2 == 1)

        def rowmax_past(b, h, t):
            sc = work.tile([P, T], F32, name="sc", bufs=6)
            a0 = small.tile([P, 1], F32, name="a0")
            past0 = (t + 1) * P if new_first(h, t) else 0
            nc.vector.tensor_scalar(
                out=sc[:, past0:past0 + S], in0=st[("sA", b, h, t)][:], scalar1=-SCALE, scalar2=None,
                op0=ALU.mult, op1=ALU.min, accum_out=a0[:],
            )
            st[("sc", b, h, t)] = sc
            st[("a0", b, h, t)] = a0

        def rowmax_new(b, h, t):
            w = (t + 1) * P
            nb = small.tile([P, 1], F32, name="nb")
            new0 = 0 if new_first(h, t) else S
            nc.vector.tensor_scalar(
                out=st[("sc", b, h, t)][:, new0:new0 + w], in0=st[("sB", b, h, t)][:, 0:w], scalar1=-SCALE,
                scalar2=st[("a0", b, h, t)][:], op0=ALU.mult, op1=ALU.min, accum_out=nb[:],
            )
            st[("nb", b, h, t)] = nb

        def expo(b, h, t):
            w = S + (t + 1) * P
            tile = (e02, e11, e02, e3)[t]
            c0 = E_COLS - w if new_first(h, t) else 0
            nc.scalar.activation(
                out=tile[:, c0:c0 + w], in_=st[("sc", b, h, t)][:, 0:w], func=ACT.Exp,
                bias=st[("nb", b, h, t)][:], scale=-1.0, accum_out=st[("rs", b, h)][:, t:t + 1],
            )

        def past_words(tile, c0):
            w = tile[:].bitcast(F32)
            return [w[:, c0 + u * P:c0 + (u + 1) * P] for u in range(2)]

        def new_words(tile):
            w = tile[:].bitcast(F32)
            return [w[:, 256 + u:512:2] for u in range(2)]

        def e_blocks(b, h, t):
            done = order[(b, h)][:order[(b, h)].index(t)]
            blocks = [("past", t, past_words((e02, e11, e02, e3)[t], 512 if new_first(h, t) else 0))]
            if t == 3:
                blocks.append(("new", 3, new_words(e3)))
            if t in (0, 2) and 2 - t in done:
                blocks.append(("new", 2, new_words(e02)))
            if t == 1 and h % 2 == 1:
                blocks.append(("new", 1, new_words(e11)))
            return blocks

        def e_pe(b, h, t):
            eT = psum.tile([P, 512], F32, name="eT", bufs=2)
            j = 0
            for kind, tt, words in e_blocks(b, h, t):
                for w in words:
                    nc.tensor.transpose(eT[:, j * P:(j + 1) * P], w, ident_f[:])
                    j += 1
            st[("eT", b, h, t)] = eT

        def e_out(b, h, t, copy_fn):
            if ("egrp", b, h) not in st:
                st[("egrp", b, h)] = work.tile([P, BLOCKS * S], BF16, name="egrp", align_bytes=64, bufs=3)
                st[("blocks", b, h)] = []
            where = st[("blocks", b, h)]
            g0 = len(where)
            for kind, tt, words in e_blocks(b, h, t):
                where.append((kind, tt))
            ng = len(where) - g0
            copy_fn(
                out=st[("egrp", b, h)][:, g0 * S:(g0 + ng) * S].bitcast(F32).rearrange(
                    "p (g m u) -> p g m u", g=ng, u=2),
                in_=st[("eT", b, h, t)][:, 0:ng * 256].rearrange("p (g u m) -> p g m u", g=ng, u=2),
            )

        def e_quant(b, h, g0, ng):
            if ("ec", b, h) not in st:
                st[("ec", b, h)] = work.tile([P, BLOCKS * P], U32, name="ec", align_bytes=64, bufs=5)
                st[("es", b, h)] = work.tile([P, BLOCKS * P], U8, name="es", align_bytes=64, bufs=5)
            nc.vector.quantize_mx(
                out=st[("ec", b, h)][:, g0 * P:(g0 + ng) * P].bitcast(FP8X4),
                scales=st[("es", b, h)][:, g0 * P:(g0 + ng) * P],
                in_=st[("egrp", b, h)][:, g0 * S:(g0 + ng) * S],
            )

        def pv_tiles(b, h, tiles, tag):
            ops = psum.tile([P, 512], F32, name="ops", tag=tag)
            full = (st[("vcodes", b)], vscales[b % 3])
            sub = vsub[b % 3]
            for j, t in enumerate(tiles):
                passes = [(h, ("past", t), full, h * P)]
                if t == 0:
                    passes.append((h, ("new", 2), sub["hi32"], h * P))
                if t == 1:
                    passes.append((h + 1 - h % 2, ("new", 1), sub["half"], h * P))
                if t == 2:
                    passes.append((h, ("new", 2), sub["lo96"], h * P))
                if t == 3:
                    passes.append((h, ("new", 3), full, (H + h) * P))
                for i, (eh, block, (vc, vs), c0) in enumerate(passes):
                    g = st[("blocks", b, eh)].index(block)
                    nc.tensor.matmul_mx(
                        out=ops[:, j * P:(j + 1) * P],
                        lhsT=st[("ec", b, eh)][:, g * P:(g + 1) * P].bitcast(FP8X4),
                        lhsT_scale=st[("es", b, eh)][:, g * P:(g + 1) * P],
                        rhs=vc[:, c0:c0 + P].bitcast(FP8X4),
                        rhs_scale=vs[:, c0:c0 + P],
                        start=(i == 0), stop=(i == 1),
                    )
            return ops

        def finish_tiles(ops, b, h, tiles, on_scalar):
            nt = len(tiles)
            ts = slice(tiles[0], tiles[-1] + 1, tiles[1] - tiles[0])
            rc = small.tile([P, NT], F32, name="rc")
            nc.gpsimd.tensor_tensor(out=rc[:, 0:nt], in0=st[("rs", b, h)][:, ts], in1=minus_one[:, 0:nt], op=ALU.pow)
            o_sb = work.tile([P, NT * P], F32, name="o_sb")
            if on_scalar:
                for i in range(nt):
                    nc.scalar.activation(
                        out=o_sb[:, i * P:(i + 1) * P], in_=ops[:, i * P:(i + 1) * P], func=ACT.Copy,
                        scale=rc[:, i:i + 1],
                    )
            else:
                nc.vector.tensor_tensor(
                    out=o_sb[:, 0:nt * P].rearrange("p (t d) -> p t d", t=nt),
                    in0=ops[:, 0:nt * P].rearrange("p (t d) -> p t d", t=nt),
                    in1=rc[:, 0:nt].unsqueeze(2).to_broadcast([P, nt, P]),
                    op=ALU.mult,
                )
            nc.sync.dma_start(
                out=out[b, :, h * P:(h + 1) * P].rearrange("(t p) d -> p t d", p=P)[:, ts],
                in_=o_sb[:, 0:nt * P].rearrange("p (t d) -> p t d", t=nt),
            )

        heads = [(b, h) for b in range(B) for h in range(H)]
        order = {hd: (0, 2, 1, 3) for hd in heads}
        order[heads[-1]] = (1, 3, 2, 0)
        steps = [(b, h, t) for (b, h) in heads for t in order[(b, h)]]
        n_steps = len(steps)
        quants = {}
        ready = {}
        for (b, h) in heads:
            last = (b, h) == heads[-1]
            first_row = steps.index((b, h, 3 if last else 1)) + QLAG
            second_row = n_steps + 1 if last else steps.index((b, h, 3)) + QLAG
            quants.setdefault(first_row, []).append((b, h, 0, 4))
            if last:
                quants.setdefault(n_steps, []).append((b, h, 4, 1))
                quants.setdefault(second_row, []).append((b, h, 5, 2))
            else:
                if h % 2 == 1:
                    quants.setdefault(first_row, []).append((b, h, 4, 1))
                quants.setdefault(second_row, []).append((b, h, 4 + h % 2, 2))
            ready[(b, h)] = (first_row, second_row)
        late_e = range(n_steps - 4, n_steps - 1)

        def warm(count):
            junk = psum.tile([P, 512], F32, name="junk", tag="sA", bufs=2)
            for i in range(count):
                nc.tensor.matmul(junk[:, 0:P], lhsT=ones_bf[:], rhs=ones_bf[:], start=True, stop=True)

        def bias_pe(tag):
            bp = psum.tile([P, 512], F32, name="bp", tag=tag)
            nc.tensor.matmul(bp[:], lhsT=ones_bf[:], rhs=bias_bf[:], start=True, stop=True)
            return bp

        value_jobs = [("x", 0, 0), ("x", 0, 1), ("bias", 0, 0)] + [("vn", 0, h) for h in range(H)]
        for b in range(1, B):
            value_jobs += [("x", b, 0), ("x", b, 1)] + [("vn", b, h) for h in range(H)]
        pv_jobs = []
        for (b, h) in heads[:-1]:
            at = ready[(b, h)][1] if h % 2 == 1 else max(ready[(b, h)][1], ready[(b, h + 1)][0])
            pv_jobs.append(("pv", b, (h, (0, 1, 2, 3), at + 1)))
        pv_jobs.append(("pv", B - 1, (H - 1, (1, 3), ready[heads[-1]][0] + 1)))
        pv_jobs.append(("pv", B - 1, (H - 1, (0, 2), ready[heads[-1]][1])))

        def job_transposes(job, n, tag, sout, early, after):
            kind, b, j = job
            if kind == "x":
                if j == 0 and b > 0:
                    batch_tiles(b)
                    for h in range(H):
                        pv_group(b, h)
                tp = words_pe(st[("x", b)], j, tag, 1)
                sout.append(lambda: words_out(tp, st[("xgrp", b)], j, nc.scalar.copy))
                if j == 1:
                    early.setdefault(n + 4, []).append(lambda: x_quant(b))
                    after.setdefault(n + 4, []).append(lambda: v_quant(b, 0))
                    st[("ready", "vn", b)] = n + 4

        def job_matmuls(job, n, tag, outs, sout, after):
            kind, b, j = job
            if kind == "bias":
                bp = bias_pe(tag)
                sout.append(lambda: nc.scalar.copy(out=bias_f[:], in_=bp[:]))
            if kind == "vn":
                vn = vnew_pe(b, j, tag)
                outs.append(lambda: vnew_out(vn, b, j))
                if j == H - 1:
                    after.setdefault(n + 2, []).append(lambda: v_quant(b, 1))
                    after.setdefault(n + 2, []).append(lambda: v_move(b))
                    st[("ready", "pv", b)] = n + 7
            if kind == "pv":
                ops = pv_tiles(b, j[0], j[1], tag)
                on_scalar = j[0] in FINISH_ON_SCALAR and b < B - 1
                (sout if on_scalar else outs).append(lambda: finish_tiles(ops, b, j[0], j[1], on_scalar))

        def next_job(n, t):
            pv_ready = False
            if pv_jobs:
                kind, b, j = pv_jobs[0]
                pv_ready = st.get(("ready", "pv", b), n_steps) <= n and j[2] <= n
            value_ready = bool(value_jobs) and min(pv_jobs[0][1] + 2, n // 16 + 1) >= value_jobs[0][1]
            if value_ready and value_jobs[0][0] == "vn":
                value_ready = st[("ready", "vn", value_jobs[0][1])] <= n
            if pv_ready and (t == 2 or not value_ready):
                return pv_jobs.pop(0)
            if value_ready:
                return value_jobs.pop(0)
            return ("none", 0, 0)

        batch_tiles(0)
        warm(28)
        q_pe(0, 0, "ops", 1)
        q_out(0, 0, nc.vector.tensor_copy)
        kT0 = headp.tile([P, T], BF16, name="kT", bufs=3)
        st[("kT", 0, 0)] = kT0
        for key, tag, bufs, c0 in (("pk", "tr", 1, 0), ("kn", "eT", 2, S)):
            half = psum.tile([P, S], BF16, name="half", tag=tag, bufs=bufs)
            half_pe(key, 0, 0, half, 0)
            nc.scalar.copy(out=kT0[:, c0:c0 + S], in_=half[:])
        scores_past(*steps[0])
        rowmax_past(*steps[0])
        scores_past(*steps[1])
        rowmax_past(*steps[1])
        scores_new(*steps[0])
        rowmax_new(*steps[0])
        scores_new(*steps[1])
        q_pe(0, 1, "ops", 1)
        q_out(0, 1, nc.vector.tensor_copy)
        k_pe(0, 1)
        k_out(0, 1)
        scores_past(*steps[2])
        rowmax_past(*steps[2])
        rowmax_new(*steps[1])
        scores_new(*steps[2])
        wt = [words_pe(w_sb, j, "eT", 2) for j in range(2)]
        for j in range(2):
            words_out(wt[j], wgrp, j, nc.scalar.copy)
        scores_past(*steps[3])
        for h in range(H):
            pv_group(0, h)

        outs = []
        sout = []
        early = {}
        after = {0: [lambda: nc.vector.quantize_mx(out=wcodes[:].bitcast(FP8X4), scales=wscales[:], in_=wgrp[:])]}
        q_wait = []
        for n in range(n_steps + 40):
            if n > n_steps and not pv_jobs and not outs:
                break
            b, h, t = steps[min(n, n_steps - 1)]
            hi = heads.index((b, h))
            t = n % NT
            for fn in early.pop(n, []):
                fn()
            for group in quants.get(n, ()):
                e_quant(*group)
            for hd in q_wait:
                q_out(*hd, nc.scalar.copy)
            q_wait = []
            now, outs = outs, []
            snow, sout = sout, []
            if 0 <= n - 1 < n_steps:
                e_pe(*steps[n - 1])
            if n < n_steps and hi + 2 < len(heads):
                if t == 1:
                    k_pe(*heads[hi + 2])
                if t == 2:
                    q_pe(*heads[hi + 2], "tr", 1)
                    q_wait.append(heads[hi + 2])
            tag = JOB_BANK[t] if n < n_steps else ("tr", "ops")[n % 2]
            if n == n_steps - 1:
                tag = None
            job = next_job(n, t) if tag else ("none", 0, 0)
            job_transposes(job, n, tag, sout, early, after)
            if n + 4 < n_steps:
                scores_past(*steps[n + 4], extra=4 if t in (1, 3) and job[0] in ("none", "x") else 0)
            job_matmuls(job, n, tag, outs, sout, after)
            if n + 3 < n_steps:
                scores_new(*steps[n + 3])
            if n < n_steps:
                expo(*steps[n])
            for fn in snow:
                fn()
            if 0 <= n - 1 < n_steps:
                e_out(*steps[n - 1], nc.vector.tensor_copy if n - 1 in late_e else nc.scalar.copy)
            if n < n_steps and hi + 2 < len(heads) and t == 1:
                k_out(*heads[hi + 2])
            if n + 3 < n_steps:
                rowmax_past(*steps[n + 3])
            for fn in now:
                fn()
            if n + 2 < n_steps:
                rowmax_new(*steps[n + 2])
            for fn in after.pop(n, []):
                fn()
            for c, s, plan in ((1, n, FIRST_LOADS), (b + 2, 4 * h + t, LATER_LOADS)):
                for what in plan.get(s, ()) if c < B and n < n_steps else ():
                    if what == "x":
                        load_tiles(c, ("x",))
                        load_x(c)
                    elif what == "pv":
                        load_tiles(c, ("pv",))
                        load_pv(c)
                    else:
                        if what == 0:
                            load_tiles(c, ("pk", "kn", "q"))
                        load_qk(c, what, what + 1)
